import numpy as np
import ml_dtypes


def mxq(x, axis, fmt="e4m3"):
    dtype, down = {"e4m3": (ml_dtypes.float8_e4m3fn, 7), "e5m2": (ml_dtypes.float8_e5m2, 14)}[fmt]
    v = np.moveaxis(np.asarray(x, np.float32).astype(ml_dtypes.bfloat16).astype(np.float64), axis, -1)
    blocks = v.reshape(v.shape[:-1] + (-1, 32))
    amax = np.abs(blocks).max(-1, keepdims=True)
    byte = np.maximum(np.where(amax > 0, np.frexp(amax)[1] - 1 + 127, 0) - down, 1)
    scale = np.exp2(byte - 127.0)
    codes = (blocks / scale).astype(np.float32).astype(dtype).astype(np.float64)
    return np.moveaxis((codes * scale).reshape(v.shape), -1, axis)


WIDE = False


def mx_kscale(k):
    if not WIDE:
        return np.ones(k)
    levels = np.array([10, -10, 5, -5, 0])
    if k % 512:
        return np.exp2(np.random.permutation(np.resize(levels, k // 32))).repeat(32)
    a = np.empty((k // 512, 16))
    for p in range(k // 512):
        a[p, :8] = np.random.permutation(np.resize(levels, 8))
        for g in range(8):
            far = levels[np.abs(levels - a[p, g]) >= 10]
            a[p, g + 8] = far[np.random.randint(len(far))]
    return np.exp2(a.ravel()).repeat(32)


BF16 = ml_dtypes.bfloat16


def bf(x):
    return np.asarray(x, np.float32).astype(BF16)


def f64(x):
    return np.asarray(x).astype(np.float64)


B, FS, NFPB, NIB, NAPB, NSPB, LOCAL, DIM, NH, RB, HG = 1, 512, 2, 3, 32, 1, 4, 1536, 12, 512, 2
HD = DIM // NH
EPS = 1e-6


def draw0():
    s = mx_kscale(DIM)
    ang = np.random.uniform(0.0, 2.0 * np.pi, (RB, HD // 2))
    return {'x': bf(np.random.standard_normal((RB, DIM)) * s),
            'w': bf(np.random.standard_normal((DIM, DIM)) / np.sqrt(DIM) / s[:, None]),
            'b': bf(np.random.standard_normal(DIM) * 0.1),
            'g': bf(1.5 + 0.15 * np.random.standard_normal(DIM)),
            'freqs': bf(np.stack([np.cos(ang), np.sin(ang)], axis=-1).reshape(RB, HD))}


def core(x, w, b, g, freqs):
    y = (mxq(f64(x), 1, 'e4m3') @ mxq(f64(w), 0, 'e4m3')) + f64(b)
    y = y * (1.0 / np.sqrt(np.mean(np.square(y), axis=-1, keepdims=True) + EPS)) * f64(g)
    yp = y.reshape(RB, NH, HD // 2, 2)
    yr, yi = yp[..., 0], yp[..., 1]
    f = f64(freqs).reshape(RB, HD // 2, 2)
    c, sn = f[:, None, :, 0], f[:, None, :, 1]
    return np.stack([yr * c - yi * sn, yr * sn + yi * c], axis=-1).reshape(RB, NH, HD)


def e4m3fn_bytes(y):
    return np.clip(np.asarray(y, np.float64), -448.0, 448.0).astype(np.float32).astype(ml_dtypes.float8_e4m3fn).view(np.uint8)


def e4m3fn_values(b):
    return np.asarray(b, np.uint8).view(ml_dtypes.float8_e4m3fn).astype(np.float64)


def setup_inputs():
    d = draw0()
    x0 = np.asarray(d['w']).astype(np.float64)
    s = (np.max(np.abs(x0), axis=(1,), keepdims=True) / 448.0).astype(np.float32)
    out = {}
    for k, v in d.items():
        if k == 'w':
            out['w_bytes'] = e4m3fn_bytes(x0 / s.astype(np.float64))
            out['w_scale'] = s
        else:
            out[k] = v
    return out


def reference(x, w_bytes, w_scale, b, g, freqs):
    return core(x, e4m3fn_values(w_bytes) * w_scale.astype(np.float64), b, g, freqs)

@@ -1,0 +1,332 @@
+from contextlib import ExitStack
+
+import concourse.mybir as mybir
+from concourse.masks import make_identity
+
+ROWS, K, N = 512, 1536, 1536
+FLOPS = 2 * ROWS * K * N
+EPS = 1e-6
+
+F32 = mybir.dt.float32
+BF16 = mybir.dt.bfloat16
+U32 = mybir.dt.uint32
+U8 = mybir.dt.uint8
+FP8 = mybir.dt.float8_e4m3fn
+FP8X4 = mybir.dt.float8_e4m3fn_x4
+ALU = mybir.AluOpType
+ACT = mybir.ActivationFunctionType
+
+P = 128
+PACK = 4
+K_PASS = P * PACK
+PASSES = K // K_PASS
+HD = 128
+HEADS = N // HD
+HALF = HD // 2
+RT = ROWS // P
+CHUNK = 256
+CHUNKS = N // CHUNK
+HPC = CHUNK // HD
+UNITS = CHUNKS * PASSES
+
+LOADS = ((0, 256), (256, 512), (512, 1024), (1024, 1536))
+LEAD = 6
+PER_SLOT = (2, 1)
+V_WIDEN_EVERY = 6
+R_LAG = 1
+E6_LAG = 2
+NORM_LATE = 5
+
+
+def tile_causalwanselfattention_pa_kernel(tc, x, w_bytes, w_scale, b, g, freqs, out):
+    nc = tc.nc
+    with ExitStack() as ctx:
+        const = ctx.enter_context(tc.tile_pool(name="const", bufs=1))
+        wide_pool = ctx.enter_context(tc.tile_pool(name="wide", bufs=4))
+        grp_pool = ctx.enter_context(tc.tile_pool(name="grp", bufs=3))
+        sq_pool = ctx.enter_context(tc.tile_pool(name="sq", bufs=3))
+        psum_y = ctx.enter_context(tc.psum_pool(name="psy", bufs=3))
+        psum_tr = ctx.enter_context(tc.psum_pool(name="pstr", bufs=4))
+        psum_s = ctx.enter_context(tc.psum_pool(name="pss", bufs=1))
+        ctx.enter_context(tc.manual_schedule())
+
+        wsc = const.tile([P, PASSES, PACK], F32, name="wsc")
+        wv = w_bytes.rearrange("(g p t) n -> g p t n", p=P, t=PACK)
+        xv = x.rearrange("(t p) k -> p t k", p=P)
+        wbytes = [
+            [const.tile([P, PACK, hi - lo], U8, name="wbytes%d_%d" % (j, i)) for i in range(PASSES)]
+            for j, (lo, hi) in enumerate(LOADS)
+        ]
+        x_sb = [const.tile([P, RT, K_PASS], BF16, name="x_sb%d" % i) for i in range(PASSES)]
+        f_sb = const.tile([P, RT, HD], BF16, name="f_sb")
+        bg_rows = const.tile([P, P], BF16, name="bg_rows")
+        nc.vector.memset(bg_rows[:], 0.0)
+
+        def load_w(j):
+            lo, hi = LOADS[j]
+            for i in range(PASSES):
+                nc.sync.dma_start(out=wbytes[j][i][:], in_=wv[i][:, :, lo:hi])
+
+        def load_x(i):
+            nc.sync.dma_start(out=x_sb[i][:], in_=xv[:, :, i * K_PASS : (i + 1) * K_PASS])
+
+        nc.sync.dma_start(out=wsc[:], in_=w_scale.rearrange("(g p t) o -> p g (t o)", p=P, t=PACK))
+        load_w(0)
+        load_x(0)
+        load_x(1)
+        load_w(1)
+        load_x(2)
+        nc.gpsimd.dma_start(out=bg_rows[0:HEADS, :], in_=b.rearrange("(h d) -> h d", d=HD))
+        nc.gpsimd.dma_start(out=bg_rows[32 : 32 + HEADS, :], in_=g.rearrange("(h d) -> h d", d=HD))
+        nc.sync.dma_start(out=f_sb[:], in_=freqs.rearrange("(t p) d -> p t d", p=P))
+        load_w(2)
+        load_w(3)
+
+        warm = const.tile([P, 2], F32, name="warm")
+        nc.vector.memset(warm[:], 1.0)
+        warm_out = const.tile([P, 2], F32, name="warm_out")
+        nc.scalar.activation(out=warm_out[:], in_=warm[:], func=ACT.Sqrt)
+
+        ident_f = const.tile([P, P], F32, name="ident_f")
+        make_identity(nc, ident_f[:])
+        ident_b = const.tile([P, P], BF16, name="ident_b")
+        make_identity(nc, ident_b[:])
+        ones2 = const.tile([P, 2], F32, name="ones2")
+        nc.vector.memset(ones2[:], 1.0)
+
+        iv = ident_f[:].rearrange("p (j e) -> p j e", e=2)
+        m_minus = const.tile([P, HALF], F32, name="m_minus")
+        m_plus = const.tile([P, HALF], F32, name="m_plus")
+        nc.gpsimd.tensor_tensor(
+            out=m_minus[:].rearrange("p (j o) -> p j o", o=1), in0=iv[:, :, 0:1], in1=iv[:, :, 1:2], op=ALU.subtract
+        )
+        nc.gpsimd.tensor_tensor(
+            out=m_plus[:].rearrange("p (j o) -> p j o", o=1), in0=iv[:, :, 0:1], in1=iv[:, :, 1:2], op=ALU.add
+        )
+
+        xcodes = const.tile([P, PASSES, ROWS], U32, name="xcodes", align_bytes=64)
+        xscales = const.tile([P, PASSES, ROWS], U8, name="xscales", align_bytes=64)
+        wcodes = const.tile([P, PASSES, N], U32, name="wcodes", align_bytes=64)
+        wscales = const.tile([P, PASSES, N], U8, name="wscales", align_bytes=64)
+
+        xgrps = {}
+
+        def x_turn(i):
+            xgrp = grp_pool.tile([P, ROWS * PACK], BF16, name="xgrp", tag="xgrp", align_bytes=64)
+            xgrps[i] = xgrp
+            xgw = xgrp[:].bitcast(F32).rearrange("p (r u) -> p r u", u=2)
+            for half in range(2):
+                xt = psum_tr.tile([P, 2, 2 * P], F32, name="xt", tag="tr")
+                for u in range(2):
+                    for s in range(2):
+                        words = x_sb[i][:, 2 * half + s, :].bitcast(F32)
+                        nc.tensor.transpose(xt[:, u, s * P : (s + 1) * P], words[:, u : 2 * P : 2], ident_f[:])
+                dst = xgw[:, 256 * half : 256 * (half + 1), :]
+                src = xt[:].rearrange("p u r -> p r u")
+                if half == 0:
+                    nc.vector.tensor_copy(out=dst, in_=src)
+                else:
+                    nc.scalar.copy(out=dst, in_=src)
+
+        def x_quant(i):
+            nc.vector.quantize_mx(out=xcodes[:, i, :].bitcast(FP8X4), scales=xscales[:, i, :], in_=xgrps[i][:])
+
+        wides = {}
+        wgrps = {}
+        count = [0]
+
+        def w_widen(u):
+            c, i = divmod(u, PASSES)
+            col = c * CHUNK
+            j = [n for n, (lo, hi) in enumerate(LOADS) if lo <= col < hi][0]
+            c0 = col - LOADS[j][0]
+            wide = wide_pool.tile([P, PACK, CHUNK], BF16, name="wide", tag="wide")
+            wides[u] = wide
+            for t in range(PACK):
+                codes = wbytes[j][i][:, t, c0 : c0 + CHUNK].bitcast(FP8)
+                count[0] += 1
+                if count[0] % V_WIDEN_EVERY == 0:
+                    nc.vector.tensor_scalar(
+                        out=wide[:, t, :], in0=codes, scalar1=wsc[:, i, t : t + 1], scalar2=None, op0=ALU.mult
+                    )
+                else:
+                    nc.scalar.activation(out=wide[:, t, :], in_=codes, func=ACT.Copy, scale=wsc[:, i, t : t + 1])
+
+        def w_weave(u):
+            wgrp = grp_pool.tile([P, CHUNK * PACK], BF16, name="wgrp", tag="wgrp", align_bytes=64)
+            wgrps[u] = wgrp
+            nc.vector.tensor_copy(
+                out=wgrp[:].rearrange("p (c t) -> p c t", t=PACK), in_=wides[u][:].rearrange("p t c -> p c t")
+            )
+
+        def w_quant(u):
+            c, i = divmod(u, PASSES)
+            cols = slice(c * CHUNK, (c + 1) * CHUNK)
+            nc.vector.quantize_mx(out=wcodes[:, i, cols].bitcast(FP8X4), scales=wscales[:, i, cols], in_=wgrps[u][:])
+
+        def w_units(first, last):
+            for u in range(first, last):
+                if u < UNITS:
+                    w_widen(u)
+                if 0 <= u - 1 < UNITS:
+                    w_weave(u - 1)
+                if 0 <= u - 2 < UNITS:
+                    w_quant(u - 2)
+
+        bgc = const.tile([P, 64], F32, name="bgc")
+        f_t = const.tile([P, ROWS], BF16, name="f_t")
+        f_t_sw = const.tile([P, ROWS], BF16, name="f_t_sw")
+        r_minus = const.tile([P, HEADS, HALF], F32, name="r_minus")
+        r_plus = const.tile([P, HEADS, HALF], F32, name="r_plus")
+
+        def tables():
+            bgt = psum_tr.tile([P, P], BF16, name="bgt", tag="tr")
+            nc.tensor.transpose(bgt[:], bg_rows[:], ident_b[:])
+            nc.vector.tensor_copy(out=bgc[:], in_=bgt[:, 0:64])
+            f_sw = const.tile([P, RT, HD], BF16, name="f_sw")
+            fv = f_sb[:].rearrange("p t (j e) -> p t j e", e=2)
+            sv = f_sw[:].rearrange("p t (j e) -> p t j e", e=2)
+            nc.gpsimd.tensor_copy(out=sv[:, :, :, 0:1], in_=fv[:, :, :, 1:2])
+            nc.gpsimd.tensor_copy(out=sv[:, :, :, 1:2], in_=fv[:, :, :, 0:1])
+            for src, dst in ((f_sb, f_t), (f_sw, f_t_sw)):
+                ft = psum_tr.tile([P, ROWS], BF16, name="ft", tag="tr")
+                for r in range(RT):
+                    nc.tensor.transpose(ft[:, r * P : (r + 1) * P], src[:, r, :], ident_b[:])
+                nc.vector.tensor_copy(out=dst[:], in_=ft[:])
+            for h in range(HEADS):
+                gcol = bgc[:, 32 + h : 33 + h]
+                nc.gpsimd.tensor_scalar(
+                    out=r_minus[:, h, :], in0=m_minus[:], scalar1=gcol, scalar2=0.0, op0=ALU.mult, op1=ALU.add
+                )
+                nc.gpsimd.tensor_scalar(
+                    out=r_plus[:, h, :], in0=m_plus[:], scalar1=gcol, scalar2=0.0, op0=ALU.mult, op1=ALU.add
+                )
+
+        ssq = psum_s.tile([P, RT, HEADS, 2], F32, name="ssq")
+        out_sb = const.tile([P, RT, N], F32, name="out_sb")
+        rstd = const.tile([P, RT], F32, name="rstd")
+        ov = out.rearrange("(t p) h d -> t p (h d)", p=P)
+        ys = {}
+        ysqs = {}
+        qs = {}
+        ros = {}
+
+        def mx(h):
+            hc = slice(h * HD, (h + 1) * HD)
+            y = psum_y.tile([P, ROWS], F32, name="y", tag="y")
+            ys[h] = y
+            for i in range(PASSES):
+                nc.tensor.matmul_mx(
+                    out=y[:],
+                    lhsT=wcodes[:, i, hc].bitcast(FP8X4),
+                    lhsT_scale=wscales[:, i, hc],
+                    rhs=xcodes[:, i, :].bitcast(FP8X4),
+                    rhs_scale=xscales[:, i, :],
+                    start=(i == 0),
+                    stop=(i == PASSES - 1),
+                )
+
+        def square(h):
+            ysq = sq_pool.tile([P, ROWS], F32, name="ysq", tag="ysq")
+            ysqs[h] = ysq
+            nc.scalar.activation(out=ysq[:], in_=ys[h][:], func=ACT.Square, bias=bgc[:, h : h + 1])
+
+        def products(h):
+            q1 = const.tile([P, ROWS], F32, name="q1_%d" % h)
+            q2 = const.tile([P, ROWS], F32, name="q2_%d" % h)
+            qs[h] = (q1, q2)
+            for q, table in ((q1, f_t), (q2, f_t_sw)):
+                nc.vector.scalar_tensor_tensor(
+                    out=q[:], in0=ys[h][:], scalar=bgc[:, h : h + 1], in1=table[:], op0=ALU.add, op1=ALU.mult
+                )
+
+        def sum_squares(h):
+            for r in range(RT):
+                nc.tensor.matmul(
+                    out=ssq[:, r, h, :], lhsT=ysqs[h][:, r * P : (r + 1) * P], rhs=ones2[:], start=True, stop=True
+                )
+
+        def rotate(h):
+            ro = psum_tr.tile([P, RT, 2, HALF], F32, name="ro", tag="tr")
+            ros[h] = ro
+            for e, table in ((0, r_minus), (1, r_plus)):
+                for r in range(RT):
+                    nc.tensor.matmul(
+                        out=ro[:, r, e, :],
+                        lhsT=qs[h][e][:, r * P : (r + 1) * P],
+                        rhs=table[:, h, :],
+                        start=True,
+                        stop=True,
+                    )
+
+        def empty(h):
+            hc = slice(h * HD, (h + 1) * HD)
+            nc.scalar.copy(
+                out=out_sb[:, :, hc].rearrange("p r (j e) -> p r j e", e=2),
+                in_=ros[h][:].rearrange("p r e j -> p r j e"),
+            )
+
+        def empty_scaled(h):
+            hc = slice(h * HD, (h + 1) * HD)
+            for r in range(RT):
+                dst = out_sb[:, r, hc].rearrange("p (j e) -> p j e", e=2)
+                src = ros[h][:, r, :, :].rearrange("p e j -> p j e")
+                if r % 2 == 0:
+                    nc.scalar.activation(out=dst, in_=src, func=ACT.Copy, scale=rstd[:, r : r + 1])
+                else:
+                    nc.vector.tensor_scalar(out=dst, in0=src, scalar1=rstd[:, r : r + 1], scalar2=None, op0=ALU.mult)
+
+        def norm_factor():
+            ssum = const.tile([P, RT], F32, name="ssum")
+            nc.vector.tensor_reduce(
+                out=ssum[:], in_=ssq[:].rearrange("p r h o -> p r (h o)"), axis=mybir.AxisListType.X, op=ALU.add
+            )
+            ms = const.tile([P, RT], F32, name="ms")
+            nc.vector.tensor_scalar(out=ms[:], in0=ssum[:], scalar1=0.5 / N, scalar2=EPS, op0=ALU.mult, op1=ALU.add)
+            sd = const.tile([P, RT], F32, name="sd")
+            nc.scalar.activation(out=sd[:], in_=ms[:], func=ACT.Sqrt)
+            nc.vector.reciprocal(out=rstd[:], in_=sd[:])
+
+        EARLY = HEADS - NORM_LATE
+        w_units(0, 2)
+        x_turn(0)
+        w_units(2, 3)
+        x_turn(1)
+        x_quant(0)
+        w_units(3, 4)
+        x_turn(2)
+        x_quant(1)
+        w_units(4, 5)
+        x_quant(2)
+        tables()
+        w_units(5, LEAD)
+        done = LEAD
+        mx(0)
+        square(0)
+        for s in range(HEADS + 3):
+            if s + 1 < HEADS:
+                mx(s + 1)
+            if s < HEADS:
+                sum_squares(s)
+                products(s)
+            if 0 <= s - R_LAG < EARLY:
+                rotate(s - R_LAG)
+            if 0 <= s - E6_LAG < EARLY:
+                empty(s - E6_LAG)
+            n_units = PER_SLOT[s % 2]
+            w_units(done, min(done + n_units, UNITS + 2))
+            done = min(done + n_units, UNITS + 2)
+            if s + 1 < HEADS:
+                square(s + 1)
+
+        norm_factor()
+        early_cols = EARLY * HD
+        for r in range(RT):
+            piece = out_sb[:, r, 0:early_cols]
+            nc.vector.tensor_scalar(out=piece, in0=piece, scalar1=rstd[:, r : r + 1], scalar2=None, op0=ALU.mult)
+            nc.sync.dma_start(out=ov[r][:, 0:early_cols], in_=piece)
+        for h in range(EARLY, HEADS):
+            rotate(h)
+            empty_scaled(h)
+        for r in range(RT):
+            nc.sync.dma_start(out=ov[r][:, early_cols:N], in_=out_sb[:, r, early_cols:N])

@@ -30,12 +30,21 @@ HPC = CHUNK // HD
 UNITS = CHUNKS * PASSES
 
 LOADS = ((0, 256), (256, 512), (512, 1024), (1024, 1536))
-LEAD = 6
-PER_SLOT = (2, 1)
-V_WIDEN_EVERY = 6
-R_LAG = 1
-E6_LAG = 2
-NORM_LATE = 5
+SQ_AT = 7
+GAIN_AT = 7
+SUM_AT = 7
+PROD_AT = 9
+X_AT = 1
+TAB_AT = 5
+X_ON_VECTOR = 1
+TABLES_ON_VECTOR = 1
+V_WIDEN_EVERY = 9
+GROUP = 4
+P_LATE = 4
+G_LATE = 2
+GAIN_ON_VECTOR = ()
+AHEAD = 3
+S_FINISH = 8
 
 
 def tile_causalwanselfattention_pa_kernel(tc, x, w_bytes, w_scale, b, g, freqs, out):
@@ -45,8 +54,9 @@ def tile_causalwanselfattention_pa_kernel(tc, x, w_bytes, w_scale, b, g, freqs, 
         wide_pool = ctx.enter_context(tc.tile_pool(name="wide", bufs=4))
         grp_pool = ctx.enter_context(tc.tile_pool(name="grp", bufs=3))
         sq_pool = ctx.enter_context(tc.tile_pool(name="sq", bufs=3))
-        psum_y = ctx.enter_context(tc.psum_pool(name="psy", bufs=3))
-        psum_tr = ctx.enter_context(tc.psum_pool(name="pstr", bufs=4))
+        z_pool = ctx.enter_context(tc.tile_pool(name="z", bufs=6))
+        psum_y = ctx.enter_context(tc.psum_pool(name="psy", bufs=4))
+        psum_tr = ctx.enter_context(tc.psum_pool(name="pstr", bufs=3))
         psum_s = ctx.enter_context(tc.psum_pool(name="pss", bufs=1))
         ctx.enter_context(tc.manual_schedule())
 
@@ -91,18 +101,11 @@ def tile_causalwanselfattention_pa_kernel(tc, x, w_bytes, w_scale, b, g, freqs, 
         make_identity(nc, ident_f[:])
         ident_b = const.tile([P, P], BF16, name="ident_b")
         make_identity(nc, ident_b[:])
-        ones2 = const.tile([P, 2], F32, name="ones2")
-        nc.vector.memset(ones2[:], 1.0)
-
+        swap_f = const.tile([P, P], F32, name="swap_f")
         iv = ident_f[:].rearrange("p (j e) -> p j e", e=2)
-        m_minus = const.tile([P, HALF], F32, name="m_minus")
-        m_plus = const.tile([P, HALF], F32, name="m_plus")
-        nc.gpsimd.tensor_tensor(
-            out=m_minus[:].rearrange("p (j o) -> p j o", o=1), in0=iv[:, :, 0:1], in1=iv[:, :, 1:2], op=ALU.subtract
-        )
-        nc.gpsimd.tensor_tensor(
-            out=m_plus[:].rearrange("p (j o) -> p j o", o=1), in0=iv[:, :, 0:1], in1=iv[:, :, 1:2], op=ALU.add
-        )
+        sw = swap_f[:].rearrange("p (j e) -> p j e", e=2)
+        nc.gpsimd.tensor_scalar(out=sw[:, :, 0:1], in0=iv[:, :, 1:2], scalar1=1.0, scalar2=0.0, op0=ALU.mult, op1=ALU.add)
+        nc.gpsimd.tensor_scalar(out=sw[:, :, 1:2], in0=iv[:, :, 0:1], scalar1=1.0, scalar2=0.0, op0=ALU.mult, op1=ALU.add)
 
         xcodes = const.tile([P, PASSES, ROWS], U32, name="xcodes", align_bytes=64)
         xscales = const.tile([P, PASSES, ROWS], U8, name="xscales", align_bytes=64)
@@ -123,7 +126,7 @@ def tile_causalwanselfattention_pa_kernel(tc, x, w_bytes, w_scale, b, g, freqs, 
                         nc.tensor.transpose(xt[:, u, s * P : (s + 1) * P], words[:, u : 2 * P : 2], ident_f[:])
                 dst = xgw[:, 256 * half : 256 * (half + 1), :]
                 src = xt[:].rearrange("p u r -> p r u")
-                if half == 0:
+                if half < X_ON_VECTOR:
                     nc.vector.tensor_copy(out=dst, in_=src)
                 else:
                     nc.scalar.copy(out=dst, in_=src)
@@ -164,60 +167,55 @@ def tile_causalwanselfattention_pa_kernel(tc, x, w_bytes, w_scale, b, g, freqs, 
             cols = slice(c * CHUNK, (c + 1) * CHUNK)
             nc.vector.quantize_mx(out=wcodes[:, i, cols].bitcast(FP8X4), scales=wscales[:, i, cols], in_=wgrps[u][:])
 
-        def w_units(first, last):
-            for u in range(first, last):
-                if u < UNITS:
-                    w_widen(u)
-                if 0 <= u - 1 < UNITS:
-                    w_weave(u - 1)
-                if 0 <= u - 2 < UNITS:
-                    w_quant(u - 2)
-
         bgc = const.tile([P, 64], F32, name="bgc")
-        f_t = const.tile([P, ROWS], BF16, name="f_t")
-        f_t_sw = const.tile([P, ROWS], BF16, name="f_t_sw")
-        r_minus = const.tile([P, HEADS, HALF], F32, name="r_minus")
-        r_plus = const.tile([P, HEADS, HALF], F32, name="r_plus")
+        bg_prod = const.tile([P, HEADS], F32, name="bg_prod")
+        cos_t = const.tile([P, ROWS], BF16, name="cos_t")
+        sin_t = const.tile([P, ROWS], BF16, name="sin_t")
 
         def tables():
             bgt = psum_tr.tile([P, P], BF16, name="bgt", tag="tr")
             nc.tensor.transpose(bgt[:], bg_rows[:], ident_b[:])
             nc.vector.tensor_copy(out=bgc[:], in_=bgt[:, 0:64])
-            f_sw = const.tile([P, RT, HD], BF16, name="f_sw")
+            nc.vector.tensor_tensor(out=bg_prod[:], in0=bgc[:, 0:HEADS], in1=bgc[:, 32 : 32 + HEADS], op=ALU.mult)
+            cos_rows = const.tile([P, RT, HD], BF16, name="cos_rows")
+            sin_rows = const.tile([P, RT, HD], BF16, name="sin_rows")
             fv = f_sb[:].rearrange("p t (j e) -> p t j e", e=2)
-            sv = f_sw[:].rearrange("p t (j e) -> p t j e", e=2)
-            nc.gpsimd.tensor_copy(out=sv[:, :, :, 0:1], in_=fv[:, :, :, 1:2])
-            nc.gpsimd.tensor_copy(out=sv[:, :, :, 1:2], in_=fv[:, :, :, 0:1])
-            for src, dst in ((f_sb, f_t), (f_sw, f_t_sw)):
+            cv = cos_rows[:].rearrange("p t (j e) -> p t j e", e=2)
+            sv = sin_rows[:].rearrange("p t (j e) -> p t j e", e=2)
+            for dst, src, sign in (
+                (cv[:, :, :, 0:1], fv[:, :, :, 0:1], 1.0),
+                (cv[:, :, :, 1:2], fv[:, :, :, 0:1], 1.0),
+                (sv[:, :, :, 0:1], fv[:, :, :, 1:2], 1.0),
+                (sv[:, :, :, 1:2], fv[:, :, :, 1:2], -1.0),
+            ):
+                nc.gpsimd.tensor_scalar(out=dst, in0=src, scalar1=sign, scalar2=0.0, op0=ALU.mult, op1=ALU.add)
+            for src, dst in ((cos_rows, cos_t), (sin_rows, sin_t)):
                 ft = psum_tr.tile([P, ROWS], BF16, name="ft", tag="tr")
                 for r in range(RT):
                     nc.tensor.transpose(ft[:, r * P : (r + 1) * P], src[:, r, :], ident_b[:])
-                nc.vector.tensor_copy(out=dst[:], in_=ft[:])
-            for h in range(HEADS):
-                gcol = bgc[:, 32 + h : 33 + h]
-                nc.gpsimd.tensor_scalar(
-                    out=r_minus[:, h, :], in0=m_minus[:], scalar1=gcol, scalar2=0.0, op0=ALU.mult, op1=ALU.add
-                )
-                nc.gpsimd.tensor_scalar(
-                    out=r_plus[:, h, :], in0=m_plus[:], scalar1=gcol, scalar2=0.0, op0=ALU.mult, op1=ALU.add
-                )
+                if TABLES_ON_VECTOR:
+                    nc.vector.tensor_copy(out=dst[:], in_=ft[:])
+                else:
+                    nc.scalar.copy(out=dst[:], in_=ft[:])
 
-        ssq = psum_s.tile([P, RT, HEADS, 2], F32, name="ssq")
+        ssq = psum_s.tile([P, RT, P], F32, name="ssq")
         out_sb = const.tile([P, RT, N], F32, name="out_sb")
         rstd = const.tile([P, RT], F32, name="rstd")
         ov = out.rearrange("(t p) h d -> t p (h d)", p=P)
         ys = {}
         ysqs = {}
+        zs = {}
         qs = {}
         ros = {}
 
-        def mx(h):
-            hc = slice(h * HD, (h + 1) * HD)
-            y = psum_y.tile([P, ROWS], F32, name="y", tag="y")
-            ys[h] = y
-            for i in range(PASSES):
+        def mx_pass(u):
+            c, i = divmod(u, PASSES)
+            for h in range(c * HPC, (c + 1) * HPC):
+                if i == 0:
+                    ys[h] = psum_y.tile([P, ROWS], F32, name="y", tag="y")
+                hc = slice(h * HD, (h + 1) * HD)
                 nc.tensor.matmul_mx(
-                    out=y[:],
+                    out=ys[h][:],
                     lhsT=wcodes[:, i, hc].bitcast(FP8X4),
                     lhsT_scale=wscales[:, i, hc],
                     rhs=xcodes[:, i, :].bitcast(FP8X4),
@@ -231,102 +229,127 @@ def tile_causalwanselfattention_pa_kernel(tc, x, w_bytes, w_scale, b, g, freqs, 
             ysqs[h] = ysq
             nc.scalar.activation(out=ysq[:], in_=ys[h][:], func=ACT.Square, bias=bgc[:, h : h + 1])
 
+        def gain(h):
+            z = z_pool.tile([P, ROWS], F32, name="z", tag="z")
+            zs[h] = z
+            gcol = bgc[:, 32 + h : 33 + h]
+            if h in GAIN_ON_VECTOR:
+                nc.vector.tensor_scalar(
+                    out=z[:], in0=ys[h][:], scalar1=gcol, scalar2=bg_prod[:, h : h + 1], op0=ALU.mult, op1=ALU.add
+                )
+            else:
+                nc.scalar.activation(out=z[:], in_=ys[h][:], func=ACT.Identity, scale=gcol, bias=bg_prod[:, h : h + 1])
+
         def products(h):
             q1 = const.tile([P, ROWS], F32, name="q1_%d" % h)
             q2 = const.tile([P, ROWS], F32, name="q2_%d" % h)
             qs[h] = (q1, q2)
-            for q, table in ((q1, f_t), (q2, f_t_sw)):
-                nc.vector.scalar_tensor_tensor(
-                    out=q[:], in0=ys[h][:], scalar=bgc[:, h : h + 1], in1=table[:], op0=ALU.add, op1=ALU.mult
-                )
+            for q, table in ((q1, cos_t), (q2, sin_t)):
+                nc.vector.tensor_tensor(out=q[:], in0=zs[h][:], in1=table[:], op=ALU.mult)
 
         def sum_squares(h):
             for r in range(RT):
                 nc.tensor.matmul(
-                    out=ssq[:, r, h, :], lhsT=ysqs[h][:, r * P : (r + 1) * P], rhs=ones2[:], start=True, stop=True
+                    out=ssq[:, r, :],
+                    lhsT=ysqs[h][:, r * P : (r + 1) * P],
+                    rhs=ident_f[:],
+                    is_transpose=True,
+                    start=(h == 0 and r == 0),
+                    stop=(h == HEADS - 1 and r == RT - 1),
                 )
 
-        def rotate(h):
-            ro = psum_tr.tile([P, RT, 2, HALF], F32, name="ro", tag="tr")
-            ros[h] = ro
-            for e, table in ((0, r_minus), (1, r_plus)):
-                for r in range(RT):
-                    nc.tensor.matmul(
-                        out=ro[:, r, e, :],
-                        lhsT=qs[h][e][:, r * P : (r + 1) * P],
-                        rhs=table[:, h, :],
-                        start=True,
-                        stop=True,
-                    )
+        def turn(dst, h, r):
+            for e, perm in ((0, ident_f), (1, swap_f)):
+                nc.tensor.matmul(
+                    out=dst,
+                    lhsT=qs[h][e][:, r * P : (r + 1) * P],
+                    rhs=perm[:],
+                    is_transpose=True,
+                    start=(e == 0),
+                    stop=(e == 1),
+                )
 
-        def empty(h):
-            hc = slice(h * HD, (h + 1) * HD)
-            nc.scalar.copy(
-                out=out_sb[:, :, hc].rearrange("p r (j e) -> p r j e", e=2),
-                in_=ros[h][:].rearrange("p r e j -> p r j e"),
-            )
+        banks = {}
 
-        def empty_scaled(h):
-            hc = slice(h * HD, (h + 1) * HD)
-            for r in range(RT):
-                dst = out_sb[:, r, hc].rearrange("p (j e) -> p j e", e=2)
-                src = ros[h][:, r, :, :].rearrange("p e j -> p j e")
-                if r % 2 == 0:
-                    nc.scalar.activation(out=dst, in_=src, func=ACT.Copy, scale=rstd[:, r : r + 1])
-                else:
-                    nc.vector.tensor_scalar(out=dst, in0=src, scalar1=rstd[:, r : r + 1], scalar2=None, op0=ALU.mult)
+        def rotate(n):
+            gq, r = divmod(n, RT)
+            bank = psum_tr.tile([P, GROUP, HD], F32, name="bank", tag="tr")
+            banks[n] = bank
+            for k in range(GROUP):
+                turn(bank[:, k, :], gq * GROUP + k, r)
 
-        def norm_factor():
-            ssum = const.tile([P, RT], F32, name="ssum")
-            nc.vector.tensor_reduce(
-                out=ssum[:], in_=ssq[:].rearrange("p r h o -> p r (h o)"), axis=mybir.AxisListType.X, op=ALU.add
-            )
-            ms = const.tile([P, RT], F32, name="ms")
-            nc.vector.tensor_scalar(out=ms[:], in0=ssum[:], scalar1=0.5 / N, scalar2=EPS, op0=ALU.mult, op1=ALU.add)
-            sd = const.tile([P, RT], F32, name="sd")
+        def finish(n):
+            gq, r = divmod(n, RT)
+            cols = slice(gq * GROUP * HD, (gq + 1) * GROUP * HD)
+            dst = out_sb[:, r, cols]
+            src = banks[n][:].rearrange("p k d -> p (k d)")
+            if n < S_FINISH or n % 2 == 0:
+                nc.scalar.activation(out=dst, in_=src, func=ACT.Copy, scale=rstd[:, r : r + 1])
+            else:
+                nc.vector.tensor_scalar(out=dst, in0=src, scalar1=rstd[:, r : r + 1], scalar2=None, op0=ALU.mult)
+            nc.sync.dma_start(out=ov[r][:, cols], in_=dst)
+
+        ssum = const.tile([P, RT], F32, name="ssum")
+        ms = const.tile([P, RT], F32, name="ms")
+        sd = const.tile([P, RT], F32, name="sd")
+
+        def norm_mean():
+            nc.vector.tensor_reduce(out=ssum[:], in_=ssq[:], axis=mybir.AxisListType.X, op=ALU.add)
+            nc.vector.tensor_scalar(out=ms[:], in0=ssum[:], scalar1=1.0 / N, scalar2=EPS, op0=ALU.mult, op1=ALU.add)
+
+        def norm_root():
             nc.scalar.activation(out=sd[:], in_=ms[:], func=ACT.Sqrt)
             nc.vector.reciprocal(out=rstd[:], in_=sd[:])
 
-        EARLY = HEADS - NORM_LATE
-        w_units(0, 2)
-        x_turn(0)
-        w_units(2, 3)
-        x_turn(1)
-        x_quant(0)
-        w_units(3, 4)
-        x_turn(2)
-        x_quant(1)
-        w_units(4, 5)
-        x_quant(2)
-        tables()
-        w_units(5, LEAD)
-        done = LEAD
-        mx(0)
-        square(0)
-        for s in range(HEADS + 3):
-            if s + 1 < HEADS:
-                mx(s + 1)
-            if s < HEADS:
-                sum_squares(s)
-                products(s)
-            if 0 <= s - R_LAG < EARLY:
-                rotate(s - R_LAG)
-            if 0 <= s - E6_LAG < EARLY:
-                empty(s - E6_LAG)
-            n_units = PER_SLOT[s % 2]
-            w_units(done, min(done + n_units, UNITS + 2))
-            done = min(done + n_units, UNITS + 2)
-            if s + 1 < HEADS:
-                square(s + 1)
+        n_banks = RT * HEADS // GROUP
+        filled = 0
 
-        norm_factor()
-        early_cols = EARLY * HD
-        for r in range(RT):
-            piece = out_sb[:, r, 0:early_cols]
-            nc.vector.tensor_scalar(out=piece, in0=piece, scalar1=rstd[:, r : r + 1], scalar2=None, op0=ALU.mult)
-            nc.sync.dma_start(out=ov[r][:, 0:early_cols], in_=piece)
-        for h in range(EARLY, HEADS):
-            rotate(h)
-            empty_scaled(h)
-        for r in range(RT):
-            nc.sync.dma_start(out=ov[r][:, early_cols:N], in_=out_sb[:, r, early_cols:N])
+        def chunk_at(u, lag):
+            c, ph = divmod(u - lag, PASSES)
+            if ph == 0 and 0 <= c < CHUNKS:
+                return list(range(c * HPC, (c + 1) * HPC))
+            return []
+
+        for u in range(UNITS + PROD_AT + 1):
+            if u < UNITS:
+                w_widen(u)
+            if 0 <= u - 1 < UNITS:
+                w_weave(u - 1)
+            if 0 <= u - X_AT < PASSES:
+                x_turn(u - X_AT)
+            if 0 <= u - 2 < UNITS - 1:
+                w_quant(u - 2)
+            if u == UNITS:
+                w_quant(UNITS - 1)
+            if 0 <= u - X_AT - 1 < PASSES:
+                x_quant(u - X_AT - 1)
+            if u == TAB_AT:
+                tables()
+            if 0 <= u - 3 < UNITS - 1:
+                mx_pass(u - 3)
+            if u == UNITS + 1:
+                mx_pass(UNITS - 1)
+            for h in chunk_at(u, SQ_AT):
+                square(h)
+            for h in chunk_at(u, GAIN_AT):
+                if h < HEADS - G_LATE:
+                    gain(h)
+            for h in chunk_at(u, SUM_AT):
+                sum_squares(h)
+            for h in chunk_at(u, PROD_AT):
+                if h < HEADS - P_LATE:
+                    products(h)
+                    while filled < min(AHEAD, RT * ((h + 1) // GROUP)):
+                        rotate(filled)
+                        filled += 1
+        norm_mean()
+        for h in range(HEADS - G_LATE, HEADS):
+            gain(h)
+        norm_root()
+        for h in range(HEADS - P_LATE, HEADS):
+            products(h)
+        for n in range(n_banks):
+            finish(n)
+            if filled < n_banks:
+                rotate(filled)
+                filled += 1

@@ -27,23 +27,30 @@ RT = ROWS // P
 CHUNK = 256
 CHUNKS = N // CHUNK
 HPC = CHUNK // HD
-UNITS = CHUNKS * PASSES
+WIDE = 512
 
-LOADS = ((0, 256), (256, 512), (512, 1024), (1024, 1536))
-SQ_AT = 7
-GAIN_AT = 7
-SUM_AT = 7
-PROD_AT = 9
-X_AT = 1
-TAB_AT = 5
-X_ON_VECTOR = 1
+UNITS = [(i, c0, WIDE) for i in range(PASSES - 1) for c0 in range(0, N, WIDE)] + [
+    (PASSES - 1, c0, CHUNK) for c0 in range(0, N, CHUNK)
+]
+FIRST = len(UNITS) - CHUNKS
+
+MX_AT = 2
+SQ_AT = 3
+GAIN_AT = 3
+SUM_AT = 4
+PROD_AT = 4
+X_AT = 4
+TAB_AT = 6
+X_ON_VECTOR = 0
 TABLES_ON_VECTOR = 1
-V_WIDEN_EVERY = 9
+V_WIDEN_EVERY = 6
 GROUP = 4
-P_LATE = 4
-G_LATE = 2
+P_LATE = 3
+G_LATE = 0
 GAIN_ON_VECTOR = ()
-AHEAD = 3
+R_AFTER_MX = 1
+EARLY_BANKS = 3
+AHEAD = 7
 S_FINISH = 8
 
 
@@ -51,46 +58,40 @@ def tile_causalwanselfattention_pa_kernel(tc, x, w_bytes, w_scale, b, g, freqs, 
     nc = tc.nc
     with ExitStack() as ctx:
         const = ctx.enter_context(tc.tile_pool(name="const", bufs=1))
-        wide_pool = ctx.enter_context(tc.tile_pool(name="wide", bufs=4))
+        wide_pool = ctx.enter_context(tc.tile_pool(name="wide", bufs=5))
         grp_pool = ctx.enter_context(tc.tile_pool(name="grp", bufs=3))
         sq_pool = ctx.enter_context(tc.tile_pool(name="sq", bufs=3))
         z_pool = ctx.enter_context(tc.tile_pool(name="z", bufs=6))
+        psum = ctx.enter_context(tc.psum_pool(name="ps", bufs=3))
         psum_y = ctx.enter_context(tc.psum_pool(name="psy", bufs=4))
-        psum_tr = ctx.enter_context(tc.psum_pool(name="pstr", bufs=3))
         psum_s = ctx.enter_context(tc.psum_pool(name="pss", bufs=1))
         ctx.enter_context(tc.manual_schedule())
 
         wsc = const.tile([P, PASSES, PACK], F32, name="wsc")
         wv = w_bytes.rearrange("(g p t) n -> g p t n", p=P, t=PACK)
         xv = x.rearrange("(t p) k -> p t k", p=P)
-        wbytes = [
-            [const.tile([P, PACK, hi - lo], U8, name="wbytes%d_%d" % (j, i)) for i in range(PASSES)]
-            for j, (lo, hi) in enumerate(LOADS)
-        ]
+        wbytes = [[const.tile([P, N], U8, name="wbytes%d_%d" % (i, t)) for t in range(PACK)] for i in range(PASSES)]
         x_sb = [const.tile([P, RT, K_PASS], BF16, name="x_sb%d" % i) for i in range(PASSES)]
         f_sb = const.tile([P, RT, HD], BF16, name="f_sb")
         bg_rows = const.tile([P, P], BF16, name="bg_rows")
         nc.vector.memset(bg_rows[:], 0.0)
 
-        def load_w(j):
-            lo, hi = LOADS[j]
-            for i in range(PASSES):
-                nc.sync.dma_start(out=wbytes[j][i][:], in_=wv[i][:, :, lo:hi])
+        def load_w(i):
+            for t in range(PACK):
+                nc.sync.dma_start(out=wbytes[i][t][:], in_=wv[i][:, t, :])
 
         def load_x(i):
             nc.sync.dma_start(out=x_sb[i][:], in_=xv[:, :, i * K_PASS : (i + 1) * K_PASS])
 
-        nc.sync.dma_start(out=wsc[:], in_=w_scale.rearrange("(g p t) o -> p g (t o)", p=P, t=PACK))
+        nc.scalar.dma_start(out=wsc[:], in_=w_scale.rearrange("(g p t) o -> p g (t o)", p=P, t=PACK))
         load_w(0)
-        load_x(0)
-        load_x(1)
         load_w(1)
-        load_x(2)
+        for i in range(PASSES):
+            load_x(i)
         nc.gpsimd.dma_start(out=bg_rows[0:HEADS, :], in_=b.rearrange("(h d) -> h d", d=HD))
         nc.gpsimd.dma_start(out=bg_rows[32 : 32 + HEADS, :], in_=g.rearrange("(h d) -> h d", d=HD))
         nc.sync.dma_start(out=f_sb[:], in_=freqs.rearrange("(t p) d -> p t d", p=P))
         load_w(2)
-        load_w(3)
 
         warm = const.tile([P, 2], F32, name="warm")
         nc.vector.memset(warm[:], 1.0)
@@ -119,7 +120,7 @@ def tile_causalwanselfattention_pa_kernel(tc, x, w_bytes, w_scale, b, g, freqs, 
             xgrps[i] = xgrp
             xgw = xgrp[:].bitcast(F32).rearrange("p (r u) -> p r u", u=2)
             for half in range(2):
-                xt = psum_tr.tile([P, 2, 2 * P], F32, name="xt", tag="tr")
+                xt = psum.tile([P, 2, 2 * P], F32, name="xt", tag="bank")
                 for u in range(2):
                     for s in range(2):
                         words = x_sb[i][:, 2 * half + s, :].bitcast(F32)
@@ -139,14 +140,11 @@ def tile_causalwanselfattention_pa_kernel(tc, x, w_bytes, w_scale, b, g, freqs, 
         count = [0]
 
         def w_widen(u):
-            c, i = divmod(u, PASSES)
-            col = c * CHUNK
-            j = [n for n, (lo, hi) in enumerate(LOADS) if lo <= col < hi][0]
-            c0 = col - LOADS[j][0]
-            wide = wide_pool.tile([P, PACK, CHUNK], BF16, name="wide", tag="wide")
+            i, c0, width = UNITS[u]
+            wide = wide_pool.tile([P, PACK, width], BF16, name="wide", tag="wide")
             wides[u] = wide
             for t in range(PACK):
-                codes = wbytes[j][i][:, t, c0 : c0 + CHUNK].bitcast(FP8)
+                codes = wbytes[i][t][:, c0 : c0 + width].bitcast(FP8)
                 count[0] += 1
                 if count[0] % V_WIDEN_EVERY == 0:
                     nc.vector.tensor_scalar(
@@ -156,15 +154,16 @@ def tile_causalwanselfattention_pa_kernel(tc, x, w_bytes, w_scale, b, g, freqs, 
                     nc.scalar.activation(out=wide[:, t, :], in_=codes, func=ACT.Copy, scale=wsc[:, i, t : t + 1])
 
         def w_weave(u):
-            wgrp = grp_pool.tile([P, CHUNK * PACK], BF16, name="wgrp", tag="wgrp", align_bytes=64)
+            width = UNITS[u][2]
+            wgrp = grp_pool.tile([P, width * PACK], BF16, name="wgrp", tag="wgrp", align_bytes=64)
             wgrps[u] = wgrp
             nc.vector.tensor_copy(
                 out=wgrp[:].rearrange("p (c t) -> p c t", t=PACK), in_=wides[u][:].rearrange("p t c -> p c t")
             )
 
         def w_quant(u):
-            c, i = divmod(u, PASSES)
-            cols = slice(c * CHUNK, (c + 1) * CHUNK)
+            i, c0, width = UNITS[u]
+            cols = slice(c0, c0 + width)
             nc.vector.quantize_mx(out=wcodes[:, i, cols].bitcast(FP8X4), scales=wscales[:, i, cols], in_=wgrps[u][:])
 
         bgc = const.tile([P, 64], F32, name="bgc")
@@ -173,7 +172,7 @@ def tile_causalwanselfattention_pa_kernel(tc, x, w_bytes, w_scale, b, g, freqs, 
         sin_t = const.tile([P, ROWS], BF16, name="sin_t")
 
         def tables():
-            bgt = psum_tr.tile([P, P], BF16, name="bgt", tag="tr")
+            bgt = psum.tile([P, P], BF16, name="bgt", tag="bank")
             nc.tensor.transpose(bgt[:], bg_rows[:], ident_b[:])
             nc.vector.tensor_copy(out=bgc[:], in_=bgt[:, 0:64])
             nc.vector.tensor_tensor(out=bg_prod[:], in0=bgc[:, 0:HEADS], in1=bgc[:, 32 : 32 + HEADS], op=ALU.mult)
@@ -190,7 +189,7 @@ def tile_causalwanselfattention_pa_kernel(tc, x, w_bytes, w_scale, b, g, freqs, 
             ):
                 nc.gpsimd.tensor_scalar(out=dst, in0=src, scalar1=sign, scalar2=0.0, op0=ALU.mult, op1=ALU.add)
             for src, dst in ((cos_rows, cos_t), (sin_rows, sin_t)):
-                ft = psum_tr.tile([P, ROWS], BF16, name="ft", tag="tr")
+                ft = psum.tile([P, ROWS], BF16, name="ft", tag="bank")
                 for r in range(RT):
                     nc.tensor.transpose(ft[:, r * P : (r + 1) * P], src[:, r, :], ident_b[:])
                 if TABLES_ON_VECTOR:
@@ -208,21 +207,21 @@ def tile_causalwanselfattention_pa_kernel(tc, x, w_bytes, w_scale, b, g, freqs, 
         qs = {}
         ros = {}
 
-        def mx_pass(u):
-            c, i = divmod(u, PASSES)
-            for h in range(c * HPC, (c + 1) * HPC):
-                if i == 0:
-                    ys[h] = psum_y.tile([P, ROWS], F32, name="y", tag="y")
-                hc = slice(h * HD, (h + 1) * HD)
-                nc.tensor.matmul_mx(
-                    out=ys[h][:],
-                    lhsT=wcodes[:, i, hc].bitcast(FP8X4),
-                    lhsT_scale=wscales[:, i, hc],
-                    rhs=xcodes[:, i, :].bitcast(FP8X4),
-                    rhs_scale=xscales[:, i, :],
-                    start=(i == 0),
-                    stop=(i == PASSES - 1),
-                )
+        def mx(c, passes):
+            for i in passes:
+                for h in range(c * HPC, (c + 1) * HPC):
+                    if i == 0:
+                        ys[h] = psum_y.tile([P, ROWS], F32, name="y", tag="y")
+                    hc = slice(h * HD, (h + 1) * HD)
+                    nc.tensor.matmul_mx(
+                        out=ys[h][:],
+                        lhsT=wcodes[:, i, hc].bitcast(FP8X4),
+                        lhsT_scale=wscales[:, i, hc],
+                        rhs=xcodes[:, i, :].bitcast(FP8X4),
+                        rhs_scale=xscales[:, i, :],
+                        start=(i == 0),
+                        stop=(i == PASSES - 1),
+                    )
 
         def square(h):
             ysq = sq_pool.tile([P, ROWS], F32, name="ysq", tag="ysq")
@@ -273,7 +272,10 @@ def tile_causalwanselfattention_pa_kernel(tc, x, w_bytes, w_scale, b, g, freqs, 
 
         def rotate(n):
             gq, r = divmod(n, RT)
-            bank = psum_tr.tile([P, GROUP, HD], F32, name="bank", tag="tr")
+            if n % AHEAD < EARLY_BANKS:
+                bank = psum.tile([P, GROUP, HD], F32, name="bank", tag="bank")
+            else:
+                bank = psum_y.tile([P, GROUP, HD], F32, name="bank_y", tag="y")
             banks[n] = bank
             for k in range(GROUP):
                 turn(bank[:, k, :], gq * GROUP + k, r)
@@ -290,62 +292,69 @@ def tile_causalwanselfattention_pa_kernel(tc, x, w_bytes, w_scale, b, g, freqs, 
             nc.sync.dma_start(out=ov[r][:, cols], in_=dst)
 
         ssum = const.tile([P, RT], F32, name="ssum")
-        ms = const.tile([P, RT], F32, name="ms")
         sd = const.tile([P, RT], F32, name="sd")
+        eps = const.tile([P, 1], F32, name="eps")
+        nc.vector.memset(eps[:], EPS)
 
-        def norm_mean():
+        def norm_factor():
             nc.vector.tensor_reduce(out=ssum[:], in_=ssq[:], axis=mybir.AxisListType.X, op=ALU.add)
-            nc.vector.tensor_scalar(out=ms[:], in0=ssum[:], scalar1=1.0 / N, scalar2=EPS, op0=ALU.mult, op1=ALU.add)
-
-        def norm_root():
-            nc.scalar.activation(out=sd[:], in_=ms[:], func=ACT.Sqrt)
+            nc.scalar.activation(out=sd[:], in_=ssum[:], func=ACT.Sqrt, scale=1.0 / N, bias=eps[:])
             nc.vector.reciprocal(out=rstd[:], in_=sd[:])
 
         n_banks = RT * HEADS // GROUP
+        n_units = len(UNITS)
         filled = 0
 
-        def chunk_at(u, lag):
-            c, ph = divmod(u - lag, PASSES)
-            if ph == 0 and 0 <= c < CHUNKS:
+        def heads_at(u, lag):
+            c = u - lag - FIRST
+            if 0 <= c < CHUNKS:
                 return list(range(c * HPC, (c + 1) * HPC))
             return []
 
-        for u in range(UNITS + PROD_AT + 1):
-            if u < UNITS:
+        for u in range(n_units + PROD_AT + 1):
+            if u < n_units:
                 w_widen(u)
-            if 0 <= u - 1 < UNITS:
+            if 0 <= u - 1 < n_units:
                 w_weave(u - 1)
             if 0 <= u - X_AT < PASSES:
                 x_turn(u - X_AT)
-            if 0 <= u - 2 < UNITS - 1:
+            if 0 <= u - 2 < n_units - 1:
                 w_quant(u - 2)
-            if u == UNITS:
-                w_quant(UNITS - 1)
+            if u == n_units:
+                w_quant(n_units - 1)
             if 0 <= u - X_AT - 1 < PASSES:
                 x_quant(u - X_AT - 1)
             if u == TAB_AT:
                 tables()
-            if 0 <= u - 3 < UNITS - 1:
-                mx_pass(u - 3)
-            if u == UNITS + 1:
-                mx_pass(UNITS - 1)
-            for h in chunk_at(u, SQ_AT):
+            for h in heads_at(u, SUM_AT):
+                sum_squares(h)
+            c = u - MX_AT - FIRST
+            if 0 <= c + 1 < CHUNKS:
+                mx(c + 1, range(PASSES - 1))
+            if 0 <= c < CHUNKS - 1:
+                mx(c, [PASSES - 1])
+            if c == CHUNKS - 2:
+                mx(CHUNKS - 1, [PASSES - 1])
+                while filled < R_AFTER_MX:
+                    rotate(filled)
+                    filled += 1
+            for h in heads_at(u, SQ_AT):
                 square(h)
-            for h in chunk_at(u, GAIN_AT):
+            for h in heads_at(u, GAIN_AT):
                 if h < HEADS - G_LATE:
                     gain(h)
-            for h in chunk_at(u, SUM_AT):
-                sum_squares(h)
-            for h in chunk_at(u, PROD_AT):
+            for h in heads_at(u, PROD_AT):
                 if h < HEADS - P_LATE:
                     products(h)
-                    while filled < min(AHEAD, RT * ((h + 1) // GROUP)):
-                        rotate(filled)
-                        filled += 1
-        norm_mean()
+        while filled < EARLY_BANKS:
+            rotate(filled)
+            filled += 1
+        norm_factor()
         for h in range(HEADS - G_LATE, HEADS):
             gain(h)
-        norm_root()
+        while filled < min(AHEAD, RT * ((HEADS - P_LATE) // GROUP)):
+            rotate(filled)
+            filled += 1
         for h in range(HEADS - P_LATE, HEADS):
             products(h)
         for n in range(n_banks):

@@ -27,30 +27,25 @@ RT = ROWS // P
 CHUNK = 256
 CHUNKS = N // CHUNK
 HPC = CHUNK // HD
-WIDE = 512
+UNITS = CHUNKS * PASSES
 
-UNITS = [(i, c0, WIDE) for i in range(PASSES - 1) for c0 in range(0, N, WIDE)] + [
-    (PASSES - 1, c0, CHUNK) for c0 in range(0, N, CHUNK)
-]
-FIRST = len(UNITS) - CHUNKS
-
-MX_AT = 2
-SQ_AT = 3
-GAIN_AT = 3
-SUM_AT = 4
-PROD_AT = 4
-X_AT = 4
-TAB_AT = 6
-X_ON_VECTOR = 0
+LOADS = ((0, 256), (256, 512), (512, 1024), (1024, 1536))
+SQ_AT = 7
+GAIN_AT = 7
+SUM_AT = 7
+PROD_AT = 9
+X_AT = 1
+TAB_AT = 5
+X_ON_VECTOR = 1
 TABLES_ON_VECTOR = 1
-V_WIDEN_EVERY = 6
+V_WIDEN_EVERY = 9
 GROUP = 4
-P_LATE = 3
+P_LATE = 4
 G_LATE = 0
 GAIN_ON_VECTOR = ()
-R_AFTER_MX = 1
 EARLY_BANKS = 3
 AHEAD = 7
+ROT_AT = (13, 14, 15, 22, 22, 23, 23)
 S_FINISH = 8
 
 
@@ -58,40 +53,46 @@ def tile_causalwanselfattention_pa_kernel(tc, x, w_bytes, w_scale, b, g, freqs, 
     nc = tc.nc
     with ExitStack() as ctx:
         const = ctx.enter_context(tc.tile_pool(name="const", bufs=1))
-        wide_pool = ctx.enter_context(tc.tile_pool(name="wide", bufs=5))
+        wide_pool = ctx.enter_context(tc.tile_pool(name="wide", bufs=4))
         grp_pool = ctx.enter_context(tc.tile_pool(name="grp", bufs=3))
         sq_pool = ctx.enter_context(tc.tile_pool(name="sq", bufs=3))
         z_pool = ctx.enter_context(tc.tile_pool(name="z", bufs=6))
-        psum = ctx.enter_context(tc.psum_pool(name="ps", bufs=3))
         psum_y = ctx.enter_context(tc.psum_pool(name="psy", bufs=4))
+        psum_tr = ctx.enter_context(tc.psum_pool(name="pstr", bufs=3))
         psum_s = ctx.enter_context(tc.psum_pool(name="pss", bufs=1))
         ctx.enter_context(tc.manual_schedule())
 
         wsc = const.tile([P, PASSES, PACK], F32, name="wsc")
         wv = w_bytes.rearrange("(g p t) n -> g p t n", p=P, t=PACK)
         xv = x.rearrange("(t p) k -> p t k", p=P)
-        wbytes = [[const.tile([P, N], U8, name="wbytes%d_%d" % (i, t)) for t in range(PACK)] for i in range(PASSES)]
+        wbytes = [
+            [const.tile([P, PACK, hi - lo], U8, name="wbytes%d_%d" % (j, i)) for i in range(PASSES)]
+            for j, (lo, hi) in enumerate(LOADS)
+        ]
         x_sb = [const.tile([P, RT, K_PASS], BF16, name="x_sb%d" % i) for i in range(PASSES)]
         f_sb = const.tile([P, RT, HD], BF16, name="f_sb")
         bg_rows = const.tile([P, P], BF16, name="bg_rows")
         nc.vector.memset(bg_rows[:], 0.0)
 
-        def load_w(i):
-            for t in range(PACK):
-                nc.sync.dma_start(out=wbytes[i][t][:], in_=wv[i][:, t, :])
+        def load_w(j):
+            lo, hi = LOADS[j]
+            for i in range(PASSES):
+                nc.sync.dma_start(out=wbytes[j][i][:], in_=wv[i][:, :, lo:hi])
 
         def load_x(i):
             nc.sync.dma_start(out=x_sb[i][:], in_=xv[:, :, i * K_PASS : (i + 1) * K_PASS])
 
-        nc.scalar.dma_start(out=wsc[:], in_=w_scale.rearrange("(g p t) o -> p g (t o)", p=P, t=PACK))
+        nc.sync.dma_start(out=wsc[:], in_=w_scale.rearrange("(g p t) o -> p g (t o)", p=P, t=PACK))
         load_w(0)
+        load_x(0)
+        load_x(1)
         load_w(1)
-        for i in range(PASSES):
-            load_x(i)
+        load_x(2)
         nc.gpsimd.dma_start(out=bg_rows[0:HEADS, :], in_=b.rearrange("(h d) -> h d", d=HD))
         nc.gpsimd.dma_start(out=bg_rows[32 : 32 + HEADS, :], in_=g.rearrange("(h d) -> h d", d=HD))
         nc.sync.dma_start(out=f_sb[:], in_=freqs.rearrange("(t p) d -> p t d", p=P))
         load_w(2)
+        load_w(3)
 
         warm = const.tile([P, 2], F32, name="warm")
         nc.vector.memset(warm[:], 1.0)
@@ -120,7 +121,7 @@ def tile_causalwanselfattention_pa_kernel(tc, x, w_bytes, w_scale, b, g, freqs, 
             xgrps[i] = xgrp
             xgw = xgrp[:].bitcast(F32).rearrange("p (r u) -> p r u", u=2)
             for half in range(2):
-                xt = psum.tile([P, 2, 2 * P], F32, name="xt", tag="bank")
+                xt = psum_tr.tile([P, 2, 2 * P], F32, name="xt", tag="tr")
                 for u in range(2):
                     for s in range(2):
                         words = x_sb[i][:, 2 * half + s, :].bitcast(F32)
@@ -140,11 +141,14 @@ def tile_causalwanselfattention_pa_kernel(tc, x, w_bytes, w_scale, b, g, freqs, 
         count = [0]
 
         def w_widen(u):
-            i, c0, width = UNITS[u]
-            wide = wide_pool.tile([P, PACK, width], BF16, name="wide", tag="wide")
+            c, i = divmod(u, PASSES)
+            col = c * CHUNK
+            j = [n for n, (lo, hi) in enumerate(LOADS) if lo <= col < hi][0]
+            c0 = col - LOADS[j][0]
+            wide = wide_pool.tile([P, PACK, CHUNK], BF16, name="wide", tag="wide")
             wides[u] = wide
             for t in range(PACK):
-                codes = wbytes[i][t][:, c0 : c0 + width].bitcast(FP8)
+                codes = wbytes[j][i][:, t, c0 : c0 + CHUNK].bitcast(FP8)
                 count[0] += 1
                 if count[0] % V_WIDEN_EVERY == 0:
                     nc.vector.tensor_scalar(
@@ -154,16 +158,15 @@ def tile_causalwanselfattention_pa_kernel(tc, x, w_bytes, w_scale, b, g, freqs, 
                     nc.scalar.activation(out=wide[:, t, :], in_=codes, func=ACT.Copy, scale=wsc[:, i, t : t + 1])
 
         def w_weave(u):
-            width = UNITS[u][2]
-            wgrp = grp_pool.tile([P, width * PACK], BF16, name="wgrp", tag="wgrp", align_bytes=64)
+            wgrp = grp_pool.tile([P, CHUNK * PACK], BF16, name="wgrp", tag="wgrp", align_bytes=64)
             wgrps[u] = wgrp
             nc.vector.tensor_copy(
                 out=wgrp[:].rearrange("p (c t) -> p c t", t=PACK), in_=wides[u][:].rearrange("p t c -> p c t")
             )
 
         def w_quant(u):
-            i, c0, width = UNITS[u]
-            cols = slice(c0, c0 + width)
+            c, i = divmod(u, PASSES)
+            cols = slice(c * CHUNK, (c + 1) * CHUNK)
             nc.vector.quantize_mx(out=wcodes[:, i, cols].bitcast(FP8X4), scales=wscales[:, i, cols], in_=wgrps[u][:])
 
         bgc = const.tile([P, 64], F32, name="bgc")
@@ -172,7 +175,7 @@ def tile_causalwanselfattention_pa_kernel(tc, x, w_bytes, w_scale, b, g, freqs, 
         sin_t = const.tile([P, ROWS], BF16, name="sin_t")
 
         def tables():
-            bgt = psum.tile([P, P], BF16, name="bgt", tag="bank")
+            bgt = psum_tr.tile([P, P], BF16, name="bgt", tag="tr")
             nc.tensor.transpose(bgt[:], bg_rows[:], ident_b[:])
             nc.vector.tensor_copy(out=bgc[:], in_=bgt[:, 0:64])
             nc.vector.tensor_tensor(out=bg_prod[:], in0=bgc[:, 0:HEADS], in1=bgc[:, 32 : 32 + HEADS], op=ALU.mult)
@@ -189,7 +192,7 @@ def tile_causalwanselfattention_pa_kernel(tc, x, w_bytes, w_scale, b, g, freqs, 
             ):
                 nc.gpsimd.tensor_scalar(out=dst, in0=src, scalar1=sign, scalar2=0.0, op0=ALU.mult, op1=ALU.add)
             for src, dst in ((cos_rows, cos_t), (sin_rows, sin_t)):
-                ft = psum.tile([P, ROWS], BF16, name="ft", tag="bank")
+                ft = psum_tr.tile([P, ROWS], BF16, name="ft", tag="tr")
                 for r in range(RT):
                     nc.tensor.transpose(ft[:, r * P : (r + 1) * P], src[:, r, :], ident_b[:])
                 if TABLES_ON_VECTOR:
@@ -207,21 +210,21 @@ def tile_causalwanselfattention_pa_kernel(tc, x, w_bytes, w_scale, b, g, freqs, 
         qs = {}
         ros = {}
 
-        def mx(c, passes):
-            for i in passes:
-                for h in range(c * HPC, (c + 1) * HPC):
-                    if i == 0:
-                        ys[h] = psum_y.tile([P, ROWS], F32, name="y", tag="y")
-                    hc = slice(h * HD, (h + 1) * HD)
-                    nc.tensor.matmul_mx(
-                        out=ys[h][:],
-                        lhsT=wcodes[:, i, hc].bitcast(FP8X4),
-                        lhsT_scale=wscales[:, i, hc],
-                        rhs=xcodes[:, i, :].bitcast(FP8X4),
-                        rhs_scale=xscales[:, i, :],
-                        start=(i == 0),
-                        stop=(i == PASSES - 1),
-                    )
+        def mx_pass(u):
+            c, i = divmod(u, PASSES)
+            for h in range(c * HPC, (c + 1) * HPC):
+                if i == 0:
+                    ys[h] = psum_y.tile([P, ROWS], F32, name="y", tag="y")
+                hc = slice(h * HD, (h + 1) * HD)
+                nc.tensor.matmul_mx(
+                    out=ys[h][:],
+                    lhsT=wcodes[:, i, hc].bitcast(FP8X4),
+                    lhsT_scale=wscales[:, i, hc],
+                    rhs=xcodes[:, i, :].bitcast(FP8X4),
+                    rhs_scale=xscales[:, i, :],
+                    start=(i == 0),
+                    stop=(i == PASSES - 1),
+                )
 
         def square(h):
             ysq = sq_pool.tile([P, ROWS], F32, name="ysq", tag="ysq")
@@ -273,7 +276,7 @@ def tile_causalwanselfattention_pa_kernel(tc, x, w_bytes, w_scale, b, g, freqs, 
         def rotate(n):
             gq, r = divmod(n, RT)
             if n % AHEAD < EARLY_BANKS:
-                bank = psum.tile([P, GROUP, HD], F32, name="bank", tag="bank")
+                bank = psum_tr.tile([P, GROUP, HD], F32, name="bank", tag="tr")
             else:
                 bank = psum_y.tile([P, GROUP, HD], F32, name="bank_y", tag="y")
             banks[n] = bank
@@ -302,57 +305,50 @@ def tile_causalwanselfattention_pa_kernel(tc, x, w_bytes, w_scale, b, g, freqs, 
             nc.vector.reciprocal(out=rstd[:], in_=sd[:])
 
         n_banks = RT * HEADS // GROUP
-        n_units = len(UNITS)
         filled = 0
 
-        def heads_at(u, lag):
-            c = u - lag - FIRST
-            if 0 <= c < CHUNKS:
+        def chunk_at(u, lag):
+            c, ph = divmod(u - lag, PASSES)
+            if ph == 0 and 0 <= c < CHUNKS:
                 return list(range(c * HPC, (c + 1) * HPC))
             return []
 
-        for u in range(n_units + PROD_AT + 1):
-            if u < n_units:
+        for u in range(UNITS + PROD_AT + 1):
+            if u < UNITS:
                 w_widen(u)
-            if 0 <= u - 1 < n_units:
+            if 0 <= u - 1 < UNITS:
                 w_weave(u - 1)
             if 0 <= u - X_AT < PASSES:
                 x_turn(u - X_AT)
-            if 0 <= u - 2 < n_units - 1:
+            if 0 <= u - 2 < UNITS - 1:
                 w_quant(u - 2)
-            if u == n_units:
-                w_quant(n_units - 1)
+            if u == UNITS:
+                w_quant(UNITS - 1)
             if 0 <= u - X_AT - 1 < PASSES:
                 x_quant(u - X_AT - 1)
             if u == TAB_AT:
                 tables()
-            for h in heads_at(u, SUM_AT):
-                sum_squares(h)
-            c = u - MX_AT - FIRST
-            if 0 <= c + 1 < CHUNKS:
-                mx(c + 1, range(PASSES - 1))
-            if 0 <= c < CHUNKS - 1:
-                mx(c, [PASSES - 1])
-            if c == CHUNKS - 2:
-                mx(CHUNKS - 1, [PASSES - 1])
-                while filled < R_AFTER_MX:
-                    rotate(filled)
-                    filled += 1
-            for h in heads_at(u, SQ_AT):
+            if 0 <= u - 3 < UNITS - 1:
+                mx_pass(u - 3)
+            if u == UNITS + 1:
+                mx_pass(UNITS - 1)
+            for h in chunk_at(u, SQ_AT):
                 square(h)
-            for h in heads_at(u, GAIN_AT):
+            for h in chunk_at(u, GAIN_AT):
                 if h < HEADS - G_LATE:
                     gain(h)
-            for h in heads_at(u, PROD_AT):
+            for h in chunk_at(u, SUM_AT):
+                sum_squares(h)
+            for h in chunk_at(u, PROD_AT):
                 if h < HEADS - P_LATE:
                     products(h)
-        while filled < EARLY_BANKS:
-            rotate(filled)
-            filled += 1
+            while filled < AHEAD and ROT_AT[filled] <= u:
+                rotate(filled)
+                filled += 1
         norm_factor()
         for h in range(HEADS - G_LATE, HEADS):
             gain(h)
-        while filled < min(AHEAD, RT * ((HEADS - P_LATE) // GROUP)):
+        while filled < AHEAD:
             rotate(filled)
             filled += 1
         for h in range(HEADS - P_LATE, HEADS):

@@ -161,7 +161,8 @@ def tile_causalwanselfattention_pa_kernel(tc, x, w_bytes, w_scale, b, g, freqs, 
             wgrp = grp_pool.tile([P, CHUNK * PACK], BF16, name="wgrp", tag="wgrp", align_bytes=64)
             wgrps[u] = wgrp
             nc.vector.tensor_copy(
-                out=wgrp[:].rearrange("p (c t) -> p c t", t=PACK), in_=wides[u][:].rearrange("p t c -> p c t")
+                out=wgrp[:].rearrange("p (c i t) -> p c t i", i=4, t=PACK),
+                in_=wides[u][:].rearrange("p t (c i) -> p c t i", i=4),
             )
 
         def w_quant(u):
@@ -295,13 +296,15 @@ def tile_causalwanselfattention_pa_kernel(tc, x, w_bytes, w_scale, b, g, freqs, 
             nc.sync.dma_start(out=ov[r][:, cols], in_=dst)
 
         ssum = const.tile([P, RT], F32, name="ssum")
+        ms = const.tile([P, RT], F32, name="ms")
         sd = const.tile([P, RT], F32, name="sd")
-        eps = const.tile([P, 1], F32, name="eps")
-        nc.vector.memset(eps[:], EPS)
 
-        def norm_factor():
+        def norm_mean():
             nc.vector.tensor_reduce(out=ssum[:], in_=ssq[:], axis=mybir.AxisListType.X, op=ALU.add)
-            nc.scalar.activation(out=sd[:], in_=ssum[:], func=ACT.Sqrt, scale=1.0 / N, bias=eps[:])
+            nc.vector.tensor_scalar(out=ms[:], in0=ssum[:], scalar1=1.0 / N, scalar2=EPS, op0=ALU.mult, op1=ALU.add)
+
+        def norm_root():
+            nc.scalar.activation(out=sd[:], in_=ms[:], func=ACT.Sqrt)
             nc.vector.reciprocal(out=rstd[:], in_=sd[:])
 
         n_banks = RT * HEADS // GROUP
@@ -345,9 +348,10 @@ def tile_causalwanselfattention_pa_kernel(tc, x, w_bytes, w_scale, b, g, freqs, 
             while filled < AHEAD and ROT_AT[filled] <= u:
                 rotate(filled)
                 filled += 1
-        norm_factor()
+        norm_mean()
         for h in range(HEADS - G_LATE, HEADS):
             gain(h)
+        norm_root()
         while filled < AHEAD:
             rotate(filled)
             filled += 1

@@ -205,6 +205,8 @@ def tile_causalwanselfattention_pa_kernel(tc, x, w_bytes, w_scale, b, g, freqs, 
         out_sb = const.tile([P, RT, N], F32, name="out_sb")
         rstd = const.tile([P, RT], F32, name="rstd")
         ov = out.rearrange("(t p) h d -> t p (h d)", p=P)
+        z_late = const.tile([P, P_LATE, ROWS], F32, name="z_late")
+        q_late = [const.tile([P, RT, P_LATE, P], F32, name="q_late%d" % e) for e in range(2)]
         ys = {}
         ysqs = {}
         zs = {}
@@ -233,22 +235,36 @@ def tile_causalwanselfattention_pa_kernel(tc, x, w_bytes, w_scale, b, g, freqs, 
             nc.scalar.activation(out=ysq[:], in_=ys[h][:], func=ACT.Square, bias=bgc[:, h : h + 1])
 
         def gain(h):
-            z = z_pool.tile([P, ROWS], F32, name="z", tag="z")
+            if h < HEADS - P_LATE:
+                z_tile = z_pool.tile([P, ROWS], F32, name="z", tag="z")
+                z = z_tile[:]
+            else:
+                z = z_late[:, h - (HEADS - P_LATE), :]
             zs[h] = z
             gcol = bgc[:, 32 + h : 33 + h]
             if h in GAIN_ON_VECTOR:
                 nc.vector.tensor_scalar(
-                    out=z[:], in0=ys[h][:], scalar1=gcol, scalar2=bg_prod[:, h : h + 1], op0=ALU.mult, op1=ALU.add
+                    out=z, in0=ys[h][:], scalar1=gcol, scalar2=bg_prod[:, h : h + 1], op0=ALU.mult, op1=ALU.add
                 )
             else:
-                nc.scalar.activation(out=z[:], in_=ys[h][:], func=ACT.Identity, scale=gcol, bias=bg_prod[:, h : h + 1])
+                nc.scalar.activation(out=z, in_=ys[h][:], func=ACT.Identity, scale=gcol, bias=bg_prod[:, h : h + 1])
 
         def products(h):
             q1 = const.tile([P, ROWS], F32, name="q1_%d" % h)
             q2 = const.tile([P, ROWS], F32, name="q2_%d" % h)
-            qs[h] = (q1, q2)
+            qs[h] = [[q[:, r * P : (r + 1) * P] for r in range(RT)] for q in (q1, q2)]
             for q, table in ((q1, cos_t), (q2, sin_t)):
-                nc.vector.tensor_tensor(out=q[:], in0=zs[h][:], in1=table[:], op=ALU.mult)
+                nc.vector.tensor_tensor(out=q[:], in0=zs[h], in1=table[:], op=ALU.mult)
+
+        def late_products(r):
+            rows = slice(r * P, (r + 1) * P)
+            for e, table in ((0, cos_t), (1, sin_t)):
+                nc.vector.tensor_tensor(
+                    out=q_late[e][:, r, :, :],
+                    in0=z_late[:, :, rows],
+                    in1=table[:, rows].unsqueeze(1).to_broadcast([P, P_LATE, P]),
+                    op=ALU.mult,
+                )
 
         def sum_squares(h):
             for r in range(RT):
@@ -265,7 +281,7 @@ def tile_causalwanselfattention_pa_kernel(tc, x, w_bytes, w_scale, b, g, freqs, 
             for e, perm in ((0, ident_f), (1, swap_f)):
                 nc.tensor.matmul(
                     out=dst,
-                    lhsT=qs[h][e][:, r * P : (r + 1) * P],
+                    lhsT=qs[h][e][r],
                     rhs=perm[:],
                     is_transpose=True,
                     start=(e == 0),
@@ -356,7 +372,9 @@ def tile_causalwanselfattention_pa_kernel(tc, x, w_bytes, w_scale, b, g, freqs, 
             rotate(filled)
             filled += 1
         for h in range(HEADS - P_LATE, HEADS):
-            products(h)
+            qs[h] = [[q_late[e][:, r, h - (HEADS - P_LATE), :] for r in range(RT)] for e in range(2)]
+        for r in range(RT):
+            late_products(r)
         for n in range(n_banks):
             finish(n)
             if filled < n_banks:

@@ -34,11 +34,13 @@ SQ_AT = 7
 GAIN_AT = 7
 SUM_AT = 7
 PROD_AT = 9
-X_AT = 1
-TAB_AT = 5
+X_AT = 3
+BG_AT = 5
+TAB_AT = 8
 X_ON_VECTOR = 1
 TABLES_ON_VECTOR = 1
 V_WIDEN_EVERY = 9
+V_UNITS = (1,)
 GROUP = 4
 P_LATE = 4
 G_LATE = 0
@@ -84,12 +86,10 @@ def tile_causalwanselfattention_pa_kernel(tc, x, w_bytes, w_scale, b, g, freqs, 
 
         nc.sync.dma_start(out=wsc[:], in_=w_scale.rearrange("(g p t) o -> p g (t o)", p=P, t=PACK))
         load_w(0)
+        load_w(1)
         load_x(0)
         load_x(1)
-        load_w(1)
         load_x(2)
-        nc.gpsimd.dma_start(out=bg_rows[0:HEADS, :], in_=b.rearrange("(h d) -> h d", d=HD))
-        nc.gpsimd.dma_start(out=bg_rows[32 : 32 + HEADS, :], in_=g.rearrange("(h d) -> h d", d=HD))
         nc.sync.dma_start(out=f_sb[:], in_=freqs.rearrange("(t p) d -> p t d", p=P))
         load_w(2)
         load_w(3)
@@ -108,6 +108,8 @@ def tile_causalwanselfattention_pa_kernel(tc, x, w_bytes, w_scale, b, g, freqs, 
         sw = swap_f[:].rearrange("p (j e) -> p j e", e=2)
         nc.gpsimd.tensor_scalar(out=sw[:, :, 0:1], in0=iv[:, :, 1:2], scalar1=1.0, scalar2=0.0, op0=ALU.mult, op1=ALU.add)
         nc.gpsimd.tensor_scalar(out=sw[:, :, 1:2], in0=iv[:, :, 0:1], scalar1=1.0, scalar2=0.0, op0=ALU.mult, op1=ALU.add)
+        nc.gpsimd.dma_start(out=bg_rows[0:HEADS, :], in_=b.rearrange("(h d) -> h d", d=HD))
+        nc.gpsimd.dma_start(out=bg_rows[32 : 32 + HEADS, :], in_=g.rearrange("(h d) -> h d", d=HD))
 
         xcodes = const.tile([P, PASSES, ROWS], U32, name="xcodes", align_bytes=64)
         xscales = const.tile([P, PASSES, ROWS], U8, name="xscales", align_bytes=64)
@@ -150,7 +152,7 @@ def tile_causalwanselfattention_pa_kernel(tc, x, w_bytes, w_scale, b, g, freqs, 
             for t in range(PACK):
                 codes = wbytes[j][i][:, t, c0 : c0 + CHUNK].bitcast(FP8)
                 count[0] += 1
-                if count[0] % V_WIDEN_EVERY == 0:
+                if u in V_UNITS or count[0] % V_WIDEN_EVERY == 0:
                     nc.vector.tensor_scalar(
                         out=wide[:, t, :], in0=codes, scalar1=wsc[:, i, t : t + 1], scalar2=None, op0=ALU.mult
                     )
@@ -175,11 +177,13 @@ def tile_causalwanselfattention_pa_kernel(tc, x, w_bytes, w_scale, b, g, freqs, 
         cos_t = const.tile([P, ROWS], BF16, name="cos_t")
         sin_t = const.tile([P, ROWS], BF16, name="sin_t")
 
-        def tables():
+        def bias_gain_columns():
             bgt = psum_tr.tile([P, P], BF16, name="bgt", tag="tr")
             nc.tensor.transpose(bgt[:], bg_rows[:], ident_b[:])
             nc.vector.tensor_copy(out=bgc[:], in_=bgt[:, 0:64])
             nc.vector.tensor_tensor(out=bg_prod[:], in0=bgc[:, 0:HEADS], in1=bgc[:, 32 : 32 + HEADS], op=ALU.mult)
+
+        def tables():
             cos_rows = const.tile([P, RT, HD], BF16, name="cos_rows")
             sin_rows = const.tile([P, RT, HD], BF16, name="sin_rows")
             fv = f_sb[:].rearrange("p t (j e) -> p t j e", e=2)
@@ -326,11 +330,17 @@ def tile_causalwanselfattention_pa_kernel(tc, x, w_bytes, w_scale, b, g, freqs, 
         n_banks = RT * HEADS // GROUP
         filled = 0
 
+        def mx_step(u):
+            if u == UNITS - 1:
+                return UNITS + 1
+            return max(u + 3, min(u + X_AT + 2, X_AT + 4 + u // 2))
+
         def chunk_at(u, lag):
-            c, ph = divmod(u - lag, PASSES)
-            if ph == 0 and 0 <= c < CHUNKS:
-                return list(range(c * HPC, (c + 1) * HPC))
-            return []
+            found = []
+            for c in range(CHUNKS):
+                if max(c * PASSES + lag, mx_step(c * PASSES + PASSES - 1) + lag - SQ_AT + 2) == u:
+                    found.extend(range(c * HPC, (c + 1) * HPC))
+            return found
 
         for u in range(UNITS + PROD_AT + 1):
             if u < UNITS:
@@ -345,12 +355,13 @@ def tile_causalwanselfattention_pa_kernel(tc, x, w_bytes, w_scale, b, g, freqs, 
                 w_quant(UNITS - 1)
             if 0 <= u - X_AT - 1 < PASSES:
                 x_quant(u - X_AT - 1)
+            if u == BG_AT:
+                bias_gain_columns()
             if u == TAB_AT:
                 tables()
-            if 0 <= u - 3 < UNITS - 1:
-                mx_pass(u - 3)
-            if u == UNITS + 1:
-                mx_pass(UNITS - 1)
+            for v in range(UNITS):
+                if mx_step(v) == u:
+                    mx_pass(v)
             for h in chunk_at(u, SQ_AT):
                 square(h)
             for h in chunk_at(u, GAIN_AT):

@@ -58,7 +58,7 @@ def tile_causalwanselfattention_pa_kernel(tc, x, w_bytes, w_scale, b, g, freqs, 
         wide_pool = ctx.enter_context(tc.tile_pool(name="wide", bufs=4))
         grp_pool = ctx.enter_context(tc.tile_pool(name="grp", bufs=3))
         sq_pool = ctx.enter_context(tc.tile_pool(name="sq", bufs=3))
-        z_pool = ctx.enter_context(tc.tile_pool(name="z", bufs=6))
+        z_pool = ctx.enter_context(tc.tile_pool(name="z", bufs=3))
         psum_y = ctx.enter_context(tc.psum_pool(name="psy", bufs=4))
         psum_tr = ctx.enter_context(tc.psum_pool(name="pstr", bufs=3))
         psum_s = ctx.enter_context(tc.psum_pool(name="pss", bufs=1))
@@ -86,8 +86,8 @@ def tile_causalwanselfattention_pa_kernel(tc, x, w_bytes, w_scale, b, g, freqs, 
 
         nc.sync.dma_start(out=wsc[:], in_=w_scale.rearrange("(g p t) o -> p g (t o)", p=P, t=PACK))
         load_w(0)
-        load_w(1)
         load_x(0)
+        load_w(1)
         load_x(1)
         load_x(2)
         nc.sync.dma_start(out=f_sb[:], in_=freqs.rearrange("(t p) d -> p t d", p=P))
@@ -174,8 +174,10 @@ def tile_causalwanselfattention_pa_kernel(tc, x, w_bytes, w_scale, b, g, freqs, 
 
         bgc = const.tile([P, 64], F32, name="bgc")
         bg_prod = const.tile([P, HEADS], F32, name="bg_prod")
-        cos_t = const.tile([P, ROWS], BF16, name="cos_t")
-        sin_t = const.tile([P, ROWS], BF16, name="sin_t")
+        tab = const.tile([P, 2, ROWS], BF16, name="tab")
+        cos_t = tab[:, 0, :]
+        sin_t = tab[:, 1, :]
+        zcs = {}
 
         def bias_gain_columns():
             bgt = psum_tr.tile([P, P], BF16, name="bgt", tag="tr")
@@ -201,9 +203,9 @@ def tile_causalwanselfattention_pa_kernel(tc, x, w_bytes, w_scale, b, g, freqs, 
                 for r in range(RT):
                     nc.tensor.transpose(ft[:, r * P : (r + 1) * P], src[:, r, :], ident_b[:])
                 if TABLES_ON_VECTOR:
-                    nc.vector.tensor_copy(out=dst[:], in_=ft[:])
+                    nc.vector.tensor_copy(out=dst, in_=ft[:])
                 else:
-                    nc.scalar.copy(out=dst[:], in_=ft[:])
+                    nc.scalar.copy(out=dst, in_=ft[:])
 
         ssq = psum_s.tile([P, RT, P], F32, name="ssq")
         out_sb = const.tile([P, RT, N], F32, name="out_sb")
@@ -240,8 +242,9 @@ def tile_causalwanselfattention_pa_kernel(tc, x, w_bytes, w_scale, b, g, freqs, 
 
         def gain(h):
             if h < HEADS - P_LATE:
-                z_tile = z_pool.tile([P, ROWS], F32, name="z", tag="z")
-                z = z_tile[:]
+                if h % HPC == 0:
+                    zcs[h // HPC] = z_pool.tile([P, HPC, ROWS], F32, name="z", tag="z")
+                z = zcs[h // HPC][:, h % HPC, :]
             else:
                 z = z_late[:, h - (HEADS - P_LATE), :]
             zs[h] = z
@@ -253,12 +256,16 @@ def tile_causalwanselfattention_pa_kernel(tc, x, w_bytes, w_scale, b, g, freqs, 
             else:
                 nc.scalar.activation(out=z, in_=ys[h][:], func=ACT.Identity, scale=gcol, bias=bg_prod[:, h : h + 1])
 
-        def products(h):
-            q1 = const.tile([P, ROWS], F32, name="q1_%d" % h)
-            q2 = const.tile([P, ROWS], F32, name="q2_%d" % h)
-            qs[h] = [[q[:, r * P : (r + 1) * P] for r in range(RT)] for q in (q1, q2)]
-            for q, table in ((q1, cos_t), (q2, sin_t)):
-                nc.vector.tensor_tensor(out=q[:], in0=zs[h], in1=table[:], op=ALU.mult)
+        def products(c):
+            q = const.tile([P, 2, HPC, ROWS], F32, name="q_%d" % c)
+            for k in range(HPC):
+                qs[c * HPC + k] = [[q[:, e, k, r * P : (r + 1) * P] for r in range(RT)] for e in range(2)]
+            nc.vector.tensor_tensor(
+                out=q[:],
+                in0=zcs[c][:].unsqueeze(1).to_broadcast([P, 2, HPC, ROWS]),
+                in1=tab[:].unsqueeze(2).to_broadcast([P, 2, HPC, ROWS]),
+                op=ALU.mult,
+            )
 
         def late_products(r):
             rows = slice(r * P, (r + 1) * P)
@@ -370,8 +377,8 @@ def tile_causalwanselfattention_pa_kernel(tc, x, w_bytes, w_scale, b, g, freqs, 
             for h in chunk_at(u, SUM_AT):
                 sum_squares(h)
             for h in chunk_at(u, PROD_AT):
-                if h < HEADS - P_LATE:
-                    products(h)
+                if h < HEADS - P_LATE and h % HPC == 0:
+                    products(h // HPC)
             while filled < AHEAD and ROT_AT[filled] <= u:
                 rotate(filled)
                 filled += 1

@@ -32,7 +32,7 @@ UNITS = CHUNKS * PASSES
 LOADS = ((0, 256), (256, 512), (512, 1024), (1024, 1536))
 SQ_AT = 7
 GAIN_AT = 7
-SUM_AT = 7
+SUM_AT = 8
 PROD_AT = 9
 X_AT = 3
 BG_AT = 5
@@ -57,7 +57,7 @@ def tile_causalwanselfattention_pa_kernel(tc, x, w_bytes, w_scale, b, g, freqs, 
         const = ctx.enter_context(tc.tile_pool(name="const", bufs=1))
         wide_pool = ctx.enter_context(tc.tile_pool(name="wide", bufs=4))
         grp_pool = ctx.enter_context(tc.tile_pool(name="grp", bufs=3))
-        sq_pool = ctx.enter_context(tc.tile_pool(name="sq", bufs=3))
+        sq_pool = ctx.enter_context(tc.tile_pool(name="sq", bufs=6))
         z_pool = ctx.enter_context(tc.tile_pool(name="z", bufs=3))
         psum_y = ctx.enter_context(tc.psum_pool(name="psy", bufs=4))
         psum_tr = ctx.enter_context(tc.psum_pool(name="pstr", bufs=3))
@@ -97,7 +97,7 @@ def tile_causalwanselfattention_pa_kernel(tc, x, w_bytes, w_scale, b, g, freqs, 
         warm = const.tile([P, 2], F32, name="warm")
         nc.vector.memset(warm[:], 1.0)
         warm_out = const.tile([P, 2], F32, name="warm_out")
-        nc.scalar.activation(out=warm_out[:], in_=warm[:], func=ACT.Sqrt)
+        nc.scalar.activation(out=warm_out[:], in_=warm[:], func=ACT.Abs_reciprocal_sqrt)
 
         ident_f = const.tile([P, P], F32, name="ident_f")
         make_identity(nc, ident_f[:])
@@ -331,8 +331,7 @@ def tile_causalwanselfattention_pa_kernel(tc, x, w_bytes, w_scale, b, g, freqs, 
             nc.vector.tensor_scalar(out=ms[:], in0=ssum[:], scalar1=1.0 / N, scalar2=EPS, op0=ALU.mult, op1=ALU.add)
 
         def norm_root():
-            nc.scalar.activation(out=sd[:], in_=ms[:], func=ACT.Sqrt)
-            nc.vector.reciprocal(out=rstd[:], in_=sd[:])
+            nc.scalar.activation(out=rstd[:], in_=ms[:], func=ACT.Abs_reciprocal_sqrt)
 
         n_banks = RT * HEADS // GROUP
         filled = 0
@@ -345,7 +344,10 @@ def tile_causalwanselfattention_pa_kernel(tc, x, w_bytes, w_scale, b, g, freqs, 
         def chunk_at(u, lag):
             found = []
             for c in range(CHUNKS):
-                if max(c * PASSES + lag, mx_step(c * PASSES + PASSES - 1) + lag - SQ_AT + 2) == u:
+                at = max(c * PASSES + lag, mx_step(c * PASSES + PASSES - 1) + lag - SQ_AT + 2)
+                if lag == SUM_AT and c == CHUNKS - 1:
+                    at -= SUM_AT - SQ_AT
+                if at == u:
                     found.extend(range(c * HPC, (c + 1) * HPC))
             return found
 

@@ -316,7 +316,7 @@ def tile_causalwanselfattention_pa_kernel(tc, x, w_bytes, w_scale, b, g, freqs, 
             cols = slice(gq * GROUP * HD, (gq + 1) * GROUP * HD)
             dst = out_sb[:, r, cols]
             src = banks[n][:].rearrange("p k d -> p (k d)")
-            if n < S_FINISH or n % 2 == 0:
+            if n != n_banks - 1:
                 nc.scalar.activation(out=dst, in_=src, func=ACT.Copy, scale=rstd[:, r : r + 1])
             else:
                 nc.vector.tensor_scalar(out=dst, in0=src, scalar1=rstd[:, r : r + 1], scalar2=None, op0=ALU.mult)

@@ -303,7 +303,9 @@ def tile_causalwanselfattention_pa_kernel(tc, x, w_bytes, w_scale, b, g, freqs, 
 
         def rotate(n):
             gq, r = divmod(n, RT)
-            if n % AHEAD < EARLY_BANKS:
+            if n == AHEAD:
+                bank = psum_s.tile([P, GROUP, HD], F32, name="bank_s", tag="ssq")
+            elif (n - n // (AHEAD + 1)) % AHEAD < EARLY_BANKS:
                 bank = psum_tr.tile([P, GROUP, HD], F32, name="bank", tag="tr")
             else:
                 bank = psum_y.tile([P, GROUP, HD], F32, name="bank_y", tag="y")
@@ -388,7 +390,7 @@ def tile_causalwanselfattention_pa_kernel(tc, x, w_bytes, w_scale, b, g, freqs, 
         for h in range(HEADS - G_LATE, HEADS):
             gain(h)
         norm_root()
-        while filled < AHEAD:
+        while filled <= AHEAD:
             rotate(filled)
             filled += 1
         for h in range(HEADS - P_LATE, HEADS):

@@ -22,7 +22,6 @@ K_PASS = P * PACK
 PASSES = K // K_PASS
 HD = 128
 HEADS = N // HD
-HALF = HD // 2
 RT = ROWS // P
 CHUNK = 256
 CHUNKS = N // CHUNK
@@ -30,25 +29,24 @@ HPC = CHUNK // HD
 UNITS = CHUNKS * PASSES
 
 LOADS = ((0, 256), (256, 512), (512, 1024), (1024, 1536))
+
 SQ_AT = 7
-GAIN_AT = 7
 SUM_AT = 8
 PROD_AT = 9
+
 X_AT = 3
 BG_AT = 5
 TAB_AT = 8
-X_ON_VECTOR = 1
-TABLES_ON_VECTOR = 1
+
+V_UNIT = 1
 V_WIDEN_EVERY = 9
-V_UNITS = (1,)
+
 GROUP = 4
-P_LATE = 4
-G_LATE = 0
-GAIN_ON_VECTOR = ()
-EARLY_BANKS = 3
-AHEAD = 7
-ROT_AT = (13, 14, 15, 22, 22, 23, 23)
-S_FINISH = 8
+BANKS = RT * HEADS // GROUP
+LATE = 4
+TR_BANKS = 3
+MX_BANKS = 4
+AHEAD = TR_BANKS + MX_BANKS
 
 
 def tile_causalwanselfattention_pa_kernel(tc, x, w_bytes, w_scale, b, g, freqs, out):
@@ -59,8 +57,8 @@ def tile_causalwanselfattention_pa_kernel(tc, x, w_bytes, w_scale, b, g, freqs, 
         grp_pool = ctx.enter_context(tc.tile_pool(name="grp", bufs=3))
         sq_pool = ctx.enter_context(tc.tile_pool(name="sq", bufs=6))
         z_pool = ctx.enter_context(tc.tile_pool(name="z", bufs=3))
-        psum_y = ctx.enter_context(tc.psum_pool(name="psy", bufs=4))
-        psum_tr = ctx.enter_context(tc.psum_pool(name="pstr", bufs=3))
+        psum_y = ctx.enter_context(tc.psum_pool(name="psy", bufs=MX_BANKS))
+        psum_tr = ctx.enter_context(tc.psum_pool(name="pstr", bufs=TR_BANKS))
         psum_s = ctx.enter_context(tc.psum_pool(name="pss", bufs=1))
         ctx.enter_context(tc.manual_schedule())
 
@@ -128,9 +126,9 @@ def tile_causalwanselfattention_pa_kernel(tc, x, w_bytes, w_scale, b, g, freqs, 
                     for s in range(2):
                         words = x_sb[i][:, 2 * half + s, :].bitcast(F32)
                         nc.tensor.transpose(xt[:, u, s * P : (s + 1) * P], words[:, u : 2 * P : 2], ident_f[:])
-                dst = xgw[:, 256 * half : 256 * (half + 1), :]
+                dst = xgw[:, 2 * P * half : 2 * P * (half + 1), :]
                 src = xt[:].rearrange("p u r -> p r u")
-                if half < X_ON_VECTOR:
+                if half == 0:
                     nc.vector.tensor_copy(out=dst, in_=src)
                 else:
                     nc.scalar.copy(out=dst, in_=src)
@@ -140,7 +138,6 @@ def tile_causalwanselfattention_pa_kernel(tc, x, w_bytes, w_scale, b, g, freqs, 
 
         wides = {}
         wgrps = {}
-        count = [0]
 
         def w_widen(u):
             c, i = divmod(u, PASSES)
@@ -151,8 +148,7 @@ def tile_causalwanselfattention_pa_kernel(tc, x, w_bytes, w_scale, b, g, freqs, 
             wides[u] = wide
             for t in range(PACK):
                 codes = wbytes[j][i][:, t, c0 : c0 + CHUNK].bitcast(FP8)
-                count[0] += 1
-                if u in V_UNITS or count[0] % V_WIDEN_EVERY == 0:
+                if u == V_UNIT or (u * PACK + t + 1) % V_WIDEN_EVERY == 0:
                     nc.vector.tensor_scalar(
                         out=wide[:, t, :], in0=codes, scalar1=wsc[:, i, t : t + 1], scalar2=None, op0=ALU.mult
                     )
@@ -175,8 +171,6 @@ def tile_causalwanselfattention_pa_kernel(tc, x, w_bytes, w_scale, b, g, freqs, 
         bgc = const.tile([P, 64], F32, name="bgc")
         bg_prod = const.tile([P, HEADS], F32, name="bg_prod")
         tab = const.tile([P, 2, ROWS], BF16, name="tab")
-        cos_t = tab[:, 0, :]
-        sin_t = tab[:, 1, :]
         zcs = {}
 
         def bias_gain_columns():
@@ -198,26 +192,21 @@ def tile_causalwanselfattention_pa_kernel(tc, x, w_bytes, w_scale, b, g, freqs, 
                 (sv[:, :, :, 1:2], fv[:, :, :, 1:2], -1.0),
             ):
                 nc.gpsimd.tensor_scalar(out=dst, in0=src, scalar1=sign, scalar2=0.0, op0=ALU.mult, op1=ALU.add)
-            for src, dst in ((cos_rows, cos_t), (sin_rows, sin_t)):
+            for e, rows_tile in ((0, cos_rows), (1, sin_rows)):
                 ft = psum_tr.tile([P, ROWS], BF16, name="ft", tag="tr")
                 for r in range(RT):
-                    nc.tensor.transpose(ft[:, r * P : (r + 1) * P], src[:, r, :], ident_b[:])
-                if TABLES_ON_VECTOR:
-                    nc.vector.tensor_copy(out=dst, in_=ft[:])
-                else:
-                    nc.scalar.copy(out=dst, in_=ft[:])
+                    nc.tensor.transpose(ft[:, r * P : (r + 1) * P], rows_tile[:, r, :], ident_b[:])
+                nc.vector.tensor_copy(out=tab[:, e, :], in_=ft[:])
 
         ssq = psum_s.tile([P, RT, P], F32, name="ssq")
         out_sb = const.tile([P, RT, N], F32, name="out_sb")
         rstd = const.tile([P, RT], F32, name="rstd")
         ov = out.rearrange("(t p) h d -> t p (h d)", p=P)
-        z_late = const.tile([P, P_LATE, ROWS], F32, name="z_late")
-        q_late = [const.tile([P, RT, P_LATE, P], F32, name="q_late%d" % e) for e in range(2)]
+        z_late = const.tile([P, LATE, ROWS], F32, name="z_late")
+        q_late = [const.tile([P, RT, LATE, P], F32, name="q_late%d" % e) for e in range(2)]
         ys = {}
         ysqs = {}
-        zs = {}
         qs = {}
-        ros = {}
 
         def mx_pass(u):
             c, i = divmod(u, PASSES)
@@ -241,20 +230,15 @@ def tile_causalwanselfattention_pa_kernel(tc, x, w_bytes, w_scale, b, g, freqs, 
             nc.scalar.activation(out=ysq[:], in_=ys[h][:], func=ACT.Square, bias=bgc[:, h : h + 1])
 
         def gain(h):
-            if h < HEADS - P_LATE:
+            if h < HEADS - LATE:
                 if h % HPC == 0:
                     zcs[h // HPC] = z_pool.tile([P, HPC, ROWS], F32, name="z", tag="z")
                 z = zcs[h // HPC][:, h % HPC, :]
             else:
-                z = z_late[:, h - (HEADS - P_LATE), :]
-            zs[h] = z
-            gcol = bgc[:, 32 + h : 33 + h]
-            if h in GAIN_ON_VECTOR:
-                nc.vector.tensor_scalar(
-                    out=z, in0=ys[h][:], scalar1=gcol, scalar2=bg_prod[:, h : h + 1], op0=ALU.mult, op1=ALU.add
-                )
-            else:
-                nc.scalar.activation(out=z, in_=ys[h][:], func=ACT.Identity, scale=gcol, bias=bg_prod[:, h : h + 1])
+                z = z_late[:, h - (HEADS - LATE), :]
+            nc.scalar.activation(
+                out=z, in_=ys[h][:], func=ACT.Identity, scale=bgc[:, 32 + h : 33 + h], bias=bg_prod[:, h : h + 1]
+            )
 
         def products(c):
             q = const.tile([P, 2, HPC, ROWS], F32, name="q_%d" % c)
@@ -269,11 +253,11 @@ def tile_causalwanselfattention_pa_kernel(tc, x, w_bytes, w_scale, b, g, freqs, 
 
         def late_products(r):
             rows = slice(r * P, (r + 1) * P)
-            for e, table in ((0, cos_t), (1, sin_t)):
+            for e in range(2):
                 nc.vector.tensor_tensor(
                     out=q_late[e][:, r, :, :],
                     in0=z_late[:, :, rows],
-                    in1=table[:, rows].unsqueeze(1).to_broadcast([P, P_LATE, P]),
+                    in1=tab[:, e, rows].unsqueeze(1).to_broadcast([P, LATE, P]),
                     op=ALU.mult,
                 )
 
@@ -288,37 +272,34 @@ def tile_causalwanselfattention_pa_kernel(tc, x, w_bytes, w_scale, b, g, freqs, 
                     stop=(h == HEADS - 1 and r == RT - 1),
                 )
 
-        def turn(dst, h, r):
-            for e, perm in ((0, ident_f), (1, swap_f)):
-                nc.tensor.matmul(
-                    out=dst,
-                    lhsT=qs[h][e][r],
-                    rhs=perm[:],
-                    is_transpose=True,
-                    start=(e == 0),
-                    stop=(e == 1),
-                )
-
         banks = {}
 
-        def rotate(n):
+        def fill(n):
             gq, r = divmod(n, RT)
             if n == AHEAD:
                 bank = psum_s.tile([P, GROUP, HD], F32, name="bank_s", tag="ssq")
-            elif (n - n // (AHEAD + 1)) % AHEAD < EARLY_BANKS:
+            elif (n - n // (AHEAD + 1)) % AHEAD < TR_BANKS:
                 bank = psum_tr.tile([P, GROUP, HD], F32, name="bank", tag="tr")
             else:
                 bank = psum_y.tile([P, GROUP, HD], F32, name="bank_y", tag="y")
             banks[n] = bank
             for k in range(GROUP):
-                turn(bank[:, k, :], gq * GROUP + k, r)
+                for e, perm in ((0, ident_f), (1, swap_f)):
+                    nc.tensor.matmul(
+                        out=bank[:, k, :],
+                        lhsT=qs[gq * GROUP + k][e][r],
+                        rhs=perm[:],
+                        is_transpose=True,
+                        start=(e == 0),
+                        stop=(e == 1),
+                    )
 
         def finish(n):
             gq, r = divmod(n, RT)
             cols = slice(gq * GROUP * HD, (gq + 1) * GROUP * HD)
             dst = out_sb[:, r, cols]
             src = banks[n][:].rearrange("p k d -> p (k d)")
-            if n != n_banks - 1:
+            if n != BANKS - 1:
                 nc.scalar.activation(out=dst, in_=src, func=ACT.Copy, scale=rstd[:, r : r + 1])
             else:
                 nc.vector.tensor_scalar(out=dst, in0=src, scalar1=rstd[:, r : r + 1], scalar2=None, op0=ALU.mult)
@@ -326,34 +307,28 @@ def tile_causalwanselfattention_pa_kernel(tc, x, w_bytes, w_scale, b, g, freqs, 
 
         ssum = const.tile([P, RT], F32, name="ssum")
         ms = const.tile([P, RT], F32, name="ms")
-        sd = const.tile([P, RT], F32, name="sd")
-
-        def norm_mean():
-            nc.vector.tensor_reduce(out=ssum[:], in_=ssq[:], axis=mybir.AxisListType.X, op=ALU.add)
-            nc.vector.tensor_scalar(out=ms[:], in0=ssum[:], scalar1=1.0 / N, scalar2=EPS, op0=ALU.mult, op1=ALU.add)
-
-        def norm_root():
-            nc.scalar.activation(out=rstd[:], in_=ms[:], func=ACT.Abs_reciprocal_sqrt)
-
-        n_banks = RT * HEADS // GROUP
-        filled = 0
 
         def mx_step(u):
             if u == UNITS - 1:
                 return UNITS + 1
             return max(u + 3, min(u + X_AT + 2, X_AT + 4 + u // 2))
 
-        def chunk_at(u, lag):
-            found = []
-            for c in range(CHUNKS):
-                at = max(c * PASSES + lag, mx_step(c * PASSES + PASSES - 1) + lag - SQ_AT + 2)
-                if lag == SUM_AT and c == CHUNKS - 1:
-                    at -= SUM_AT - SQ_AT
-                if at == u:
-                    found.extend(range(c * HPC, (c + 1) * HPC))
-            return found
+        def stage_step(c, lag):
+            at = max(c * PASSES + lag, mx_step(c * PASSES + PASSES - 1) + lag - SQ_AT + 2)
+            if lag == SUM_AT and c == CHUNKS - 1:
+                at -= SUM_AT - SQ_AT
+            return at
 
-        for u in range(UNITS + PROD_AT + 1):
+        def heads_at(u, lag):
+            return [h for c in range(CHUNKS) if stage_step(c, lag) == u for h in range(c * HPC, (c + 1) * HPC)]
+
+        def fill_step(n):
+            if n < TR_BANKS:
+                return stage_step(GROUP // HPC - 1, PROD_AT) + n
+            return stage_step(CHUNKS - 1, SQ_AT) + (n - TR_BANKS) // 2
+
+        filled = 0
+        for u in range(fill_step(AHEAD - 1) + 1):
             if u < UNITS:
                 w_widen(u)
             if 0 <= u - 1 < UNITS:
@@ -373,32 +348,31 @@ def tile_causalwanselfattention_pa_kernel(tc, x, w_bytes, w_scale, b, g, freqs, 
             for v in range(UNITS):
                 if mx_step(v) == u:
                     mx_pass(v)
-            for h in chunk_at(u, SQ_AT):
+            for h in heads_at(u, SQ_AT):
                 square(h)
-            for h in chunk_at(u, GAIN_AT):
-                if h < HEADS - G_LATE:
-                    gain(h)
-            for h in chunk_at(u, SUM_AT):
+            for h in heads_at(u, SQ_AT):
+                gain(h)
+            for h in heads_at(u, SUM_AT):
                 sum_squares(h)
-            for h in chunk_at(u, PROD_AT):
-                if h < HEADS - P_LATE and h % HPC == 0:
+            for h in heads_at(u, PROD_AT):
+                if h < HEADS - LATE and h % HPC == 0:
                     products(h // HPC)
-            while filled < AHEAD and ROT_AT[filled] <= u:
-                rotate(filled)
+            while filled < AHEAD and fill_step(filled) <= u:
+                fill(filled)
                 filled += 1
-        norm_mean()
-        for h in range(HEADS - G_LATE, HEADS):
-            gain(h)
-        norm_root()
-        while filled <= AHEAD:
-            rotate(filled)
-            filled += 1
-        for h in range(HEADS - P_LATE, HEADS):
-            qs[h] = [[q_late[e][:, r, h - (HEADS - P_LATE), :] for r in range(RT)] for e in range(2)]
+
+        nc.vector.tensor_reduce(out=ssum[:], in_=ssq[:], axis=mybir.AxisListType.X, op=ALU.add)
+        nc.vector.tensor_scalar(out=ms[:], in0=ssum[:], scalar1=1.0 / N, scalar2=EPS, op0=ALU.mult, op1=ALU.add)
+        nc.scalar.activation(out=rstd[:], in_=ms[:], func=ACT.Abs_reciprocal_sqrt)
+
+        fill(filled)
+        filled += 1
+        for h in range(HEADS - LATE, HEADS):
+            qs[h] = [[q_late[e][:, r, h - (HEADS - LATE), :] for r in range(RT)] for e in range(2)]
         for r in range(RT):
             late_products(r)
-        for n in range(n_banks):
+        for n in range(BANKS):
             finish(n)
-            if filled < n_banks:
-                rotate(filled)
+            if filled < BANKS:
+                fill(filled)
                 filled += 1

@@ -35,7 +35,7 @@ SUM_AT = 8
 PROD_AT = 9
 
 X_AT = 3
-BG_AT = 5
+BG_AT = 2
 TAB_AT = 8
 
 V_UNIT = 1
@@ -73,6 +73,10 @@ def tile_causalwanselfattention_pa_kernel(tc, x, w_bytes, w_scale, b, g, freqs, 
         f_sb = const.tile([P, RT, HD], BF16, name="f_sb")
         bg_rows = const.tile([P, P], BF16, name="bg_rows")
         nc.vector.memset(bg_rows[:], 0.0)
+        for vec, row0 in ((b, 0), (g, 32)):
+            vrows = vec.rearrange("(h d) -> h d", d=HD)
+            for lo, hi in ((0, 8), (8, HEADS)):
+                nc.scalar.dma_start(out=bg_rows[row0 + lo : row0 + hi, :], in_=vrows[lo:hi, :])
 
         def load_w(j):
             lo, hi = LOADS[j]
@@ -106,8 +110,15 @@ def tile_causalwanselfattention_pa_kernel(tc, x, w_bytes, w_scale, b, g, freqs, 
         sw = swap_f[:].rearrange("p (j e) -> p j e", e=2)
         nc.gpsimd.tensor_scalar(out=sw[:, :, 0:1], in0=iv[:, :, 1:2], scalar1=1.0, scalar2=0.0, op0=ALU.mult, op1=ALU.add)
         nc.gpsimd.tensor_scalar(out=sw[:, :, 1:2], in0=iv[:, :, 0:1], scalar1=1.0, scalar2=0.0, op0=ALU.mult, op1=ALU.add)
-        nc.gpsimd.dma_start(out=bg_rows[0:HEADS, :], in_=b.rearrange("(h d) -> h d", d=HD))
-        nc.gpsimd.dma_start(out=bg_rows[32 : 32 + HEADS, :], in_=g.rearrange("(h d) -> h d", d=HD))
+        sel = [const.tile([P, P], BF16, name="sel%d" % e) for e in range(2)]
+        ib = ident_b[:].rearrange("p (j e) -> p j e", e=2)
+        for e in range(2):
+            se = sel[e][:].rearrange("p (j e) -> p j e", e=2)
+            for col in range(2):
+                sign = -1.0 if e == 1 and col == 1 else 1.0
+                nc.gpsimd.tensor_scalar(
+                    out=se[:, :, col : col + 1], in0=ib[:, :, e : e + 1], scalar1=sign, scalar2=0.0, op0=ALU.mult, op1=ALU.add
+                )
 
         xcodes = const.tile([P, PASSES, ROWS], U32, name="xcodes", align_bytes=64)
         xscales = const.tile([P, PASSES, ROWS], U8, name="xscales", align_bytes=64)
@@ -179,24 +190,19 @@ def tile_causalwanselfattention_pa_kernel(tc, x, w_bytes, w_scale, b, g, freqs, 
             nc.vector.tensor_copy(out=bgc[:], in_=bgt[:, 0:64])
             nc.vector.tensor_tensor(out=bg_prod[:], in0=bgc[:, 0:HEADS], in1=bgc[:, 32 : 32 + HEADS], op=ALU.mult)
 
+        f_turned = const.tile([P, ROWS], BF16, name="f_turned")
+
+        def turn_freqs():
+            ft = psum_tr.tile([P, ROWS], BF16, name="ft", tag="tr")
+            for r in range(RT):
+                nc.tensor.transpose(ft[:, r * P : (r + 1) * P], f_sb[:, r, :], ident_b[:])
+            nc.vector.tensor_copy(out=f_turned[:], in_=ft[:])
+
         def tables():
-            cos_rows = const.tile([P, RT, HD], BF16, name="cos_rows")
-            sin_rows = const.tile([P, RT, HD], BF16, name="sin_rows")
-            fv = f_sb[:].rearrange("p t (j e) -> p t j e", e=2)
-            cv = cos_rows[:].rearrange("p t (j e) -> p t j e", e=2)
-            sv = sin_rows[:].rearrange("p t (j e) -> p t j e", e=2)
-            for dst, src, sign in (
-                (cv[:, :, :, 0:1], fv[:, :, :, 0:1], 1.0),
-                (cv[:, :, :, 1:2], fv[:, :, :, 0:1], 1.0),
-                (sv[:, :, :, 0:1], fv[:, :, :, 1:2], 1.0),
-                (sv[:, :, :, 1:2], fv[:, :, :, 1:2], -1.0),
-            ):
-                nc.gpsimd.tensor_scalar(out=dst, in0=src, scalar1=sign, scalar2=0.0, op0=ALU.mult, op1=ALU.add)
-            for e, rows_tile in ((0, cos_rows), (1, sin_rows)):
-                ft = psum_tr.tile([P, ROWS], BF16, name="ft", tag="tr")
-                for r in range(RT):
-                    nc.tensor.transpose(ft[:, r * P : (r + 1) * P], rows_tile[:, r, :], ident_b[:])
-                nc.vector.tensor_copy(out=tab[:, e, :], in_=ft[:])
+            for e in range(2):
+                tt = psum_tr.tile([P, ROWS], BF16, name="tt", tag="tr")
+                nc.tensor.matmul(out=tt[:], lhsT=sel[e][:], rhs=f_turned[:], start=True, stop=True)
+                nc.vector.tensor_copy(out=tab[:, e, :], in_=tt[:])
 
         ssq = psum_s.tile([P, RT, P], F32, name="ssq")
         out_sb = const.tile([P, RT, N], F32, name="out_sb")
@@ -333,6 +339,8 @@ def tile_causalwanselfattention_pa_kernel(tc, x, w_bytes, w_scale, b, g, freqs, 
                 w_widen(u)
             if 0 <= u - 1 < UNITS:
                 w_weave(u - 1)
+            if u == BG_AT:
+                bias_gain_columns()
             if 0 <= u - X_AT < PASSES:
                 x_turn(u - X_AT)
             if 0 <= u - 2 < UNITS - 1:
@@ -341,8 +349,8 @@ def tile_causalwanselfattention_pa_kernel(tc, x, w_bytes, w_scale, b, g, freqs, 
                 w_quant(UNITS - 1)
             if 0 <= u - X_AT - 1 < PASSES:
                 x_quant(u - X_AT - 1)
-            if u == BG_AT:
-                bias_gain_columns()
+            if u == TAB_AT - 1:
+                turn_freqs()
             if u == TAB_AT:
                 tables()
             for v in range(UNITS):

@@ -23,30 +23,32 @@ PASSES = K // K_PASS
 HD = 128
 HEADS = N // HD
 RT = ROWS // P
-CHUNK = 256
-CHUNKS = N // CHUNK
-HPC = CHUNK // HD
+WIDTHS = (512, 512, 256, 256)
+STARTS = tuple(sum(WIDTHS[:c]) for c in range(len(WIDTHS)))
+CHUNKS = len(WIDTHS)
 UNITS = CHUNKS * PASSES
 
-LOADS = ((0, 256), (256, 512), (512, 1024), (1024, 1536))
+LOADS = ((0, 512), (512, 1024), (1024, 1536))
 
-SQ_AT = 7
-SUM_AT = 8
-PROD_AT = 9
-
-X_AT = 3
+X_AT = 2
 BG_AT = 2
-TAB_AT = 8
+TAB_AT = 6
+SQ_AT = (5, 5, 6, 7, 8, 9, 10, 11, 12, 12, 13, 13)
+PROD_AT = (7, 9, 12)
+SLOTS = 14
 
-V_UNIT = 1
-V_WIDEN_EVERY = 9
+V_FIRST = 3
+V_WIDEN_EVERY = 7
 
 GROUP = 4
 BANKS = RT * HEADS // GROUP
+PAIR = 2
 LATE = 4
+MID = 2
 TR_BANKS = 3
 MX_BANKS = 4
 AHEAD = TR_BANKS + MX_BANKS
+READY = RT
 
 
 def tile_causalwanselfattention_pa_kernel(tc, x, w_bytes, w_scale, b, g, freqs, out):
@@ -69,32 +71,34 @@ def tile_causalwanselfattention_pa_kernel(tc, x, w_bytes, w_scale, b, g, freqs, 
             [const.tile([P, PACK, hi - lo], U8, name="wbytes%d_%d" % (j, i)) for i in range(PASSES)]
             for j, (lo, hi) in enumerate(LOADS)
         ]
-        x_sb = [const.tile([P, RT, K_PASS], BF16, name="x_sb%d" % i) for i in range(PASSES)]
+        x_sb = [const.tile([P, 2, K], BF16, name="x_sb%d" % half) for half in range(2)]
         f_sb = const.tile([P, RT, HD], BF16, name="f_sb")
         bg_rows = const.tile([P, P], BF16, name="bg_rows")
         nc.vector.memset(bg_rows[:], 0.0)
-        for vec, row0 in ((b, 0), (g, 32)):
-            vrows = vec.rearrange("(h d) -> h d", d=HD)
-            for lo, hi in ((0, 8), (8, HEADS)):
-                nc.scalar.dma_start(out=bg_rows[row0 + lo : row0 + hi, :], in_=vrows[lo:hi, :])
 
-        def load_w(j):
+        def load_bg():
+            for vec, row0 in ((b, 0), (g, 32)):
+                vrows = vec.rearrange("(h d) -> h d", d=HD)
+                for lo, hi in ((0, 8), (8, HEADS)):
+                    nc.sync.dma_start(out=bg_rows[row0 + lo : row0 + hi, :], in_=vrows[lo:hi, :])
+
+        def load_w(j, first=0, end=PASSES):
             lo, hi = LOADS[j]
-            for i in range(PASSES):
+            for i in range(first, end):
                 nc.sync.dma_start(out=wbytes[j][i][:], in_=wv[i][:, :, lo:hi])
 
-        def load_x(i):
-            nc.sync.dma_start(out=x_sb[i][:], in_=xv[:, :, i * K_PASS : (i + 1) * K_PASS])
+        def load_x(half):
+            nc.sync.dma_start(out=x_sb[half][:], in_=xv[:, 2 * half : 2 * half + 2, :])
 
         nc.sync.dma_start(out=wsc[:], in_=w_scale.rearrange("(g p t) o -> p g (t o)", p=P, t=PACK))
         load_w(0)
+        load_bg()
         load_x(0)
-        load_w(1)
+        load_w(1, 0, 1)
         load_x(1)
-        load_x(2)
         nc.sync.dma_start(out=f_sb[:], in_=freqs.rearrange("(t p) d -> p t d", p=P))
+        load_w(1, 1, PASSES)
         load_w(2)
-        load_w(3)
 
         warm = const.tile([P, 2], F32, name="warm")
         nc.vector.memset(warm[:], 1.0)
@@ -125,18 +129,16 @@ def tile_causalwanselfattention_pa_kernel(tc, x, w_bytes, w_scale, b, g, freqs, 
         wcodes = const.tile([P, PASSES, N], U32, name="wcodes", align_bytes=64)
         wscales = const.tile([P, PASSES, N], U8, name="wscales", align_bytes=64)
 
-        xgrps = {}
+        xgrps = [const.tile([P, ROWS * PACK], BF16, name="xgrp%d" % i, align_bytes=64) for i in range(PASSES)]
 
-        def x_turn(i):
-            xgrp = grp_pool.tile([P, ROWS * PACK], BF16, name="xgrp", tag="xgrp", align_bytes=64)
-            xgrps[i] = xgrp
-            xgw = xgrp[:].bitcast(F32).rearrange("p (r u) -> p r u", u=2)
-            for half in range(2):
+        def x_turn(half):
+            for i in range(PASSES):
                 xt = psum_tr.tile([P, 2, 2 * P], F32, name="xt", tag="tr")
                 for u in range(2):
                     for s in range(2):
-                        words = x_sb[i][:, 2 * half + s, :].bitcast(F32)
+                        words = x_sb[half][:, s, i * K_PASS : (i + 1) * K_PASS].bitcast(F32)
                         nc.tensor.transpose(xt[:, u, s * P : (s + 1) * P], words[:, u : 2 * P : 2], ident_f[:])
+                xgw = xgrps[i][:].bitcast(F32).rearrange("p (r u) -> p r u", u=2)
                 dst = xgw[:, 2 * P * half : 2 * P * (half + 1), :]
                 src = xt[:].rearrange("p u r -> p r u")
                 if half == 0:
@@ -150,16 +152,20 @@ def tile_causalwanselfattention_pa_kernel(tc, x, w_bytes, w_scale, b, g, freqs, 
         wides = {}
         wgrps = {}
 
-        def w_widen(u):
+        def unit_columns(u):
             c, i = divmod(u, PASSES)
-            col = c * CHUNK
-            j = [n for n, (lo, hi) in enumerate(LOADS) if lo <= col < hi][0]
-            c0 = col - LOADS[j][0]
-            wide = wide_pool.tile([P, PACK, CHUNK], BF16, name="wide", tag="wide")
+            return i, slice(STARTS[c], STARTS[c] + WIDTHS[c])
+
+        def w_widen(u):
+            i, cols = unit_columns(u)
+            width = cols.stop - cols.start
+            j = [n for n, (lo, hi) in enumerate(LOADS) if lo <= cols.start < hi][0]
+            c0 = cols.start - LOADS[j][0]
+            wide = wide_pool.tile([P, PACK, width], BF16, name="wide", tag="wide")
             wides[u] = wide
             for t in range(PACK):
-                codes = wbytes[j][i][:, t, c0 : c0 + CHUNK].bitcast(FP8)
-                if u == V_UNIT or (u * PACK + t + 1) % V_WIDEN_EVERY == 0:
+                codes = wbytes[j][i][:, t, c0 : c0 + width].bitcast(FP8)
+                if (u == 0 and t >= PACK - V_FIRST) or (u > 0 and (u * PACK + t + 1) % V_WIDEN_EVERY == 0):
                     nc.vector.tensor_scalar(
                         out=wide[:, t, :], in0=codes, scalar1=wsc[:, i, t : t + 1], scalar2=None, op0=ALU.mult
                     )
@@ -167,7 +173,8 @@ def tile_causalwanselfattention_pa_kernel(tc, x, w_bytes, w_scale, b, g, freqs, 
                     nc.scalar.activation(out=wide[:, t, :], in_=codes, func=ACT.Copy, scale=wsc[:, i, t : t + 1])
 
         def w_weave(u):
-            wgrp = grp_pool.tile([P, CHUNK * PACK], BF16, name="wgrp", tag="wgrp", align_bytes=64)
+            i, cols = unit_columns(u)
+            wgrp = grp_pool.tile([P, (cols.stop - cols.start) * PACK], BF16, name="wgrp", tag="wgrp", align_bytes=64)
             wgrps[u] = wgrp
             nc.vector.tensor_copy(
                 out=wgrp[:].rearrange("p (c i t) -> p c t i", i=4, t=PACK),
@@ -175,8 +182,7 @@ def tile_causalwanselfattention_pa_kernel(tc, x, w_bytes, w_scale, b, g, freqs, 
             )
 
         def w_quant(u):
-            c, i = divmod(u, PASSES)
-            cols = slice(c * CHUNK, (c + 1) * CHUNK)
+            i, cols = unit_columns(u)
             nc.vector.quantize_mx(out=wcodes[:, i, cols].bitcast(FP8X4), scales=wscales[:, i, cols], in_=wgrps[u][:])
 
         bgc = const.tile([P, 64], F32, name="bgc")
@@ -192,11 +198,16 @@ def tile_causalwanselfattention_pa_kernel(tc, x, w_bytes, w_scale, b, g, freqs, 
 
         f_turned = const.tile([P, ROWS], BF16, name="f_turned")
 
+        fts = []
+
         def turn_freqs():
             ft = psum_tr.tile([P, ROWS], BF16, name="ft", tag="tr")
+            fts.append(ft)
             for r in range(RT):
                 nc.tensor.transpose(ft[:, r * P : (r + 1) * P], f_sb[:, r, :], ident_b[:])
-            nc.vector.tensor_copy(out=f_turned[:], in_=ft[:])
+
+        def copy_freqs():
+            nc.vector.tensor_copy(out=f_turned[:], in_=fts[0][:])
 
         def tables():
             for e in range(2):
@@ -212,23 +223,22 @@ def tile_causalwanselfattention_pa_kernel(tc, x, w_bytes, w_scale, b, g, freqs, 
         q_late = [const.tile([P, RT, LATE, P], F32, name="q_late%d" % e) for e in range(2)]
         ys = {}
         ysqs = {}
+        q_pair = {}
         qs = {}
 
-        def mx_pass(u):
-            c, i = divmod(u, PASSES)
-            for h in range(c * HPC, (c + 1) * HPC):
-                if i == 0:
-                    ys[h] = psum_y.tile([P, ROWS], F32, name="y", tag="y")
-                hc = slice(h * HD, (h + 1) * HD)
-                nc.tensor.matmul_mx(
-                    out=ys[h][:],
-                    lhsT=wcodes[:, i, hc].bitcast(FP8X4),
-                    lhsT_scale=wscales[:, i, hc],
-                    rhs=xcodes[:, i, :].bitcast(FP8X4),
-                    rhs_scale=xscales[:, i, :],
-                    start=(i == 0),
-                    stop=(i == PASSES - 1),
-                )
+        def mx_pass(h, i):
+            if i == 0:
+                ys[h] = psum_y.tile([P, ROWS], F32, name="y", tag="y")
+            hc = slice(h * HD, (h + 1) * HD)
+            nc.tensor.matmul_mx(
+                out=ys[h][:],
+                lhsT=wcodes[:, i, hc].bitcast(FP8X4),
+                lhsT_scale=wscales[:, i, hc],
+                rhs=xcodes[:, i, :].bitcast(FP8X4),
+                rhs_scale=xscales[:, i, :],
+                start=(i == 0),
+                stop=(i == PASSES - 1),
+            )
 
         def square(h):
             ysq = sq_pool.tile([P, ROWS], F32, name="ysq", tag="ysq")
@@ -237,23 +247,24 @@ def tile_causalwanselfattention_pa_kernel(tc, x, w_bytes, w_scale, b, g, freqs, 
 
         def gain(h):
             if h < HEADS - LATE:
-                if h % HPC == 0:
-                    zcs[h // HPC] = z_pool.tile([P, HPC, ROWS], F32, name="z", tag="z")
-                z = zcs[h // HPC][:, h % HPC, :]
+                if h % PAIR == 0:
+                    zcs[h // PAIR] = z_pool.tile([P, PAIR, ROWS], F32, name="z", tag="z")
+                z = zcs[h // PAIR][:, h % PAIR, :]
             else:
                 z = z_late[:, h - (HEADS - LATE), :]
-            nc.scalar.activation(
-                out=z, in_=ys[h][:], func=ACT.Identity, scale=bgc[:, 32 + h : 33 + h], bias=bg_prod[:, h : h + 1]
-            )
+            gcol, bgcol = bgc[:, 32 + h : 33 + h], bg_prod[:, h : h + 1]
+            nc.scalar.activation(out=z, in_=ys[h][:], func=ACT.Identity, scale=gcol, bias=bgcol)
 
-        def products(c):
-            q = const.tile([P, 2, HPC, ROWS], F32, name="q_%d" % c)
-            for k in range(HPC):
-                qs[c * HPC + k] = [[q[:, e, k, r * P : (r + 1) * P] for r in range(RT)] for e in range(2)]
+        def products(c, lo=0, hi=ROWS):
+            if lo == 0:
+                q = const.tile([P, 2, PAIR, ROWS], F32, name="q_%d" % c)
+                q_pair[c] = q
+                for k in range(PAIR):
+                    qs[c * PAIR + k] = [[q[:, e, k, r * P : (r + 1) * P] for r in range(RT)] for e in range(2)]
             nc.vector.tensor_tensor(
-                out=q[:],
-                in0=zcs[c][:].unsqueeze(1).to_broadcast([P, 2, HPC, ROWS]),
-                in1=tab[:].unsqueeze(2).to_broadcast([P, 2, HPC, ROWS]),
+                out=q_pair[c][:, :, :, lo:hi],
+                in0=zcs[c][:, :, lo:hi].unsqueeze(1).to_broadcast([P, 2, PAIR, hi - lo]),
+                in1=tab[:, :, lo:hi].unsqueeze(2).to_broadcast([P, 2, PAIR, hi - lo]),
                 op=ALU.mult,
             )
 
@@ -280,19 +291,19 @@ def tile_causalwanselfattention_pa_kernel(tc, x, w_bytes, w_scale, b, g, freqs, 
 
         banks = {}
 
-        def fill(n):
+        def fill(n, first=0, end=GROUP):
             gq, r = divmod(n, RT)
-            if n == AHEAD:
-                bank = psum_s.tile([P, GROUP, HD], F32, name="bank_s", tag="ssq")
-            elif (n - n // (AHEAD + 1)) % AHEAD < TR_BANKS:
-                bank = psum_tr.tile([P, GROUP, HD], F32, name="bank", tag="tr")
-            else:
-                bank = psum_y.tile([P, GROUP, HD], F32, name="bank_y", tag="y")
-            banks[n] = bank
-            for k in range(GROUP):
+            if first == 0:
+                if n == AHEAD:
+                    banks[n] = psum_s.tile([P, GROUP, HD], F32, name="bank_s", tag="ssq")
+                elif (n - n // (AHEAD + 1)) % AHEAD < TR_BANKS:
+                    banks[n] = psum_tr.tile([P, GROUP, HD], F32, name="bank", tag="tr")
+                else:
+                    banks[n] = psum_y.tile([P, GROUP, HD], F32, name="bank_y", tag="y")
+            for k in range(first, end):
                 for e, perm in ((0, ident_f), (1, swap_f)):
                     nc.tensor.matmul(
-                        out=bank[:, k, :],
+                        out=banks[n][:, k, :],
                         lhsT=qs[gq * GROUP + k][e][r],
                         rhs=perm[:],
                         is_transpose=True,
@@ -314,72 +325,86 @@ def tile_causalwanselfattention_pa_kernel(tc, x, w_bytes, w_scale, b, g, freqs, 
         ssum = const.tile([P, RT], F32, name="ssum")
         ms = const.tile([P, RT], F32, name="ms")
 
-        def mx_step(u):
-            if u == UNITS - 1:
-                return UNITS + 1
-            return max(u + 3, min(u + X_AT + 2, X_AT + 4 + u // 2))
+        def chunk_heads(c):
+            return range(STARTS[c] // HD, (STARTS[c] + WIDTHS[c]) // HD)
 
-        def stage_step(c, lag):
-            at = max(c * PASSES + lag, mx_step(c * PASSES + PASSES - 1) + lag - SQ_AT + 2)
-            if lag == SUM_AT and c == CHUNKS - 1:
-                at -= SUM_AT - SQ_AT
-            return at
-
-        def heads_at(u, lag):
-            return [h for c in range(CHUNKS) if stage_step(c, lag) == u for h in range(c * HPC, (c + 1) * HPC)]
-
-        def fill_step(n):
-            if n < TR_BANKS:
-                return stage_step(GROUP // HPC - 1, PROD_AT) + n
-            return stage_step(CHUNKS - 1, SQ_AT) + (n - TR_BANKS) // 2
-
-        filled = 0
-        for u in range(fill_step(AHEAD - 1) + 1):
+        for u in range(SLOTS):
             if u < UNITS:
                 w_widen(u)
             if 0 <= u - 1 < UNITS:
                 w_weave(u - 1)
             if u == BG_AT:
                 bias_gain_columns()
-            if 0 <= u - X_AT < PASSES:
+            if 0 <= u - X_AT < 2:
                 x_turn(u - X_AT)
-            if 0 <= u - 2 < UNITS - 1:
+            if 0 <= u - 2 < UNITS - 1 and u - 2 != PASSES - 1:
                 w_quant(u - 2)
+            if u == X_AT + 1:
+                for i in range(PASSES):
+                    x_quant(i)
+                w_quant(PASSES - 1)
             if u == UNITS:
                 w_quant(UNITS - 1)
-            if 0 <= u - X_AT - 1 < PASSES:
-                x_quant(u - X_AT - 1)
-            if u == TAB_AT - 1:
+            if u == TAB_AT - 2:
                 turn_freqs()
+            if u == TAB_AT - 1:
+                copy_freqs()
             if u == TAB_AT:
                 tables()
-            for v in range(UNITS):
-                if mx_step(v) == u:
-                    mx_pass(v)
-            for h in heads_at(u, SQ_AT):
+            for c in range(CHUNKS):
+                if u == (PASSES * c + PASSES + 1 if c < CHUNKS - 1 else UNITS):
+                    if c == 1:
+                        for h in chunk_heads(c):
+                            for i in range(PASSES):
+                                mx_pass(h, i)
+                    else:
+                        for i in range(PASSES):
+                            for h in chunk_heads(c):
+                                mx_pass(h, i)
+            heads = [h for h in range(HEADS) if SQ_AT[h] == u]
+            for h in heads:
                 square(h)
-            for h in heads_at(u, SQ_AT):
+            for h in heads:
                 gain(h)
-            for h in heads_at(u, SUM_AT):
-                sum_squares(h)
-            for h in heads_at(u, PROD_AT):
-                if h < HEADS - LATE and h % HPC == 0:
-                    products(h // HPC)
-            while filled < AHEAD and fill_step(filled) <= u:
-                fill(filled)
-                filled += 1
+            for h in range(HEADS):
+                if min(SQ_AT[h] + 1, SLOTS - 1) == u:
+                    sum_squares(h)
+            for p, at in enumerate(PROD_AT):
+                if at == u:
+                    products(p)
+                    if p == len(PROD_AT) - 1:
+                        products(p + 1, 0, P)
+            if u == SLOTS - 1:
+                products(len(PROD_AT), P, 2 * P)
+            if u == PROD_AT[1]:
+                for n in range(TR_BANKS):
+                    fill(n, 0, PAIR)
+            if u == UNITS:
+                for n in range(TR_BANKS):
+                    fill(n, PAIR, GROUP)
+        for n in range(TR_BANKS, READY):
+            fill(n)
+        filled = READY
 
-        nc.vector.tensor_reduce(out=ssum[:], in_=ssq[:], axis=mybir.AxisListType.X, op=ALU.add)
-        nc.vector.tensor_scalar(out=ms[:], in0=ssum[:], scalar1=1.0 / N, scalar2=EPS, op0=ALU.mult, op1=ALU.add)
-        nc.scalar.activation(out=rstd[:], in_=ms[:], func=ACT.Abs_reciprocal_sqrt)
+        for lo, hi in ((0, 1), (1, RT)):
+            nc.vector.tensor_reduce(out=ssum[:, lo:hi], in_=ssq[:, lo:hi, :], axis=mybir.AxisListType.X, op=ALU.add)
+            nc.vector.tensor_scalar(out=ms[:, lo:hi], in0=ssum[:, lo:hi], scalar1=1.0 / N, scalar2=EPS, op0=ALU.mult, op1=ALU.add)
+            nc.scalar.activation(out=rstd[:, lo:hi], in_=ms[:, lo:hi], func=ACT.Abs_reciprocal_sqrt)
+            if lo == 0:
+                finish(0)
 
-        fill(filled)
-        filled += 1
         for h in range(HEADS - LATE, HEADS):
             qs[h] = [[q_late[e][:, r, h - (HEADS - LATE), :] for r in range(RT)] for e in range(2)]
+        for r in range(2, RT):
+            products(len(PROD_AT), r * P, (r + 1) * P)
         for r in range(RT):
             late_products(r)
-        for n in range(BANKS):
+        while filled < AHEAD + 1:
+            fill(filled)
+            filled += 1
+        fill(filled)
+        filled += 1
+        for n in range(1, BANKS):
             finish(n)
             if filled < BANKS:
                 fill(filled)

@@ -37,8 +37,7 @@ SQ_AT = (5, 5, 6, 7, 8, 9, 10, 11, 12, 12, 13, 13)
 PROD_AT = (7, 9, 12)
 SLOTS = 14
 
-V_FIRST = 3
-V_WIDEN_EVERY = 7
+V_WIDEN_EVERY = 6
 
 GROUP = 4
 BANKS = RT * HEADS // GROUP
@@ -85,7 +84,8 @@ def tile_causalwanselfattention_pa_kernel(tc, x, w_bytes, w_scale, b, g, freqs, 
         def load_w(j, first=0, end=PASSES):
             lo, hi = LOADS[j]
             for i in range(first, end):
-                nc.sync.dma_start(out=wbytes[j][i][:], in_=wv[i][:, :, lo:hi])
+                for t0, t1 in ((0, 2), (2, PACK)) if (j, i) == (0, 0) else ((0, PACK),):
+                    nc.sync.dma_start(out=wbytes[j][i][:, t0:t1, :], in_=wv[i][:, t0:t1, lo:hi])
 
         def load_x(half):
             nc.sync.dma_start(out=x_sb[half][:], in_=xv[:, 2 * half : 2 * half + 2, :])
@@ -165,7 +165,7 @@ def tile_causalwanselfattention_pa_kernel(tc, x, w_bytes, w_scale, b, g, freqs, 
             wides[u] = wide
             for t in range(PACK):
                 codes = wbytes[j][i][:, t, c0 : c0 + width].bitcast(FP8)
-                if (u == 0 and t >= PACK - V_FIRST) or (u > 0 and (u * PACK + t + 1) % V_WIDEN_EVERY == 0):
+                if (u == 0 and t > 0) or (u > 0 and (u * PACK + t + 1) % V_WIDEN_EVERY == 0):
                     nc.vector.tensor_scalar(
                         out=wide[:, t, :], in0=codes, scalar1=wsc[:, i, t : t + 1], scalar2=None, op0=ALU.mult
                     )
@@ -313,17 +313,19 @@ def tile_causalwanselfattention_pa_kernel(tc, x, w_bytes, w_scale, b, g, freqs, 
 
         def finish(n):
             gq, r = divmod(n, RT)
-            cols = slice(gq * GROUP * HD, (gq + 1) * GROUP * HD)
-            dst = out_sb[:, r, cols]
-            src = banks[n][:].rearrange("p k d -> p (k d)")
-            if n != BANKS - 1:
-                nc.scalar.activation(out=dst, in_=src, func=ACT.Copy, scale=rstd[:, r : r + 1])
-            else:
-                nc.vector.tensor_scalar(out=dst, in0=src, scalar1=rstd[:, r : r + 1], scalar2=None, op0=ALU.mult)
-            nc.sync.dma_start(out=ov[r][:, cols], in_=dst)
+            for lo, hi in ((0, PAIR), (PAIR, GROUP)) if n == 0 else ((0, GROUP),):
+                cols = slice((gq * GROUP + lo) * HD, (gq * GROUP + hi) * HD)
+                dst = out_sb[:, r, cols]
+                src = banks[n][:, lo:hi, :].rearrange("p k d -> p (k d)")
+                if n != BANKS - 1:
+                    nc.scalar.activation(out=dst, in_=src, func=ACT.Copy, scale=rstd[:, r : r + 1])
+                else:
+                    nc.vector.tensor_scalar(out=dst, in0=src, scalar1=rstd[:, r : r + 1], scalar2=None, op0=ALU.mult)
+                nc.sync.dma_start(out=ov[r][:, cols], in_=dst)
 
         ssum = const.tile([P, RT], F32, name="ssum")
-        ms = const.tile([P, RT], F32, name="ms")
+        eps_col = const.tile([P, 1], F32, name="eps_col")
+        nc.vector.memset(eps_col[:], EPS)
 
         def chunk_heads(c):
             return range(STARTS[c] // HD, (STARTS[c] + WIDTHS[c]) // HD)
@@ -380,16 +382,18 @@ def tile_causalwanselfattention_pa_kernel(tc, x, w_bytes, w_scale, b, g, freqs, 
                 for n in range(TR_BANKS):
                     fill(n, 0, PAIR)
             if u == UNITS:
-                for n in range(TR_BANKS):
-                    fill(n, PAIR, GROUP)
+                fill(0, PAIR, GROUP)
+        for n in range(1, TR_BANKS):
+            fill(n, PAIR, GROUP)
         for n in range(TR_BANKS, READY):
             fill(n)
         filled = READY
 
         for lo, hi in ((0, 1), (1, RT)):
             nc.vector.tensor_reduce(out=ssum[:, lo:hi], in_=ssq[:, lo:hi, :], axis=mybir.AxisListType.X, op=ALU.add)
-            nc.vector.tensor_scalar(out=ms[:, lo:hi], in0=ssum[:, lo:hi], scalar1=1.0 / N, scalar2=EPS, op0=ALU.mult, op1=ALU.add)
-            nc.scalar.activation(out=rstd[:, lo:hi], in_=ms[:, lo:hi], func=ACT.Abs_reciprocal_sqrt)
+            nc.scalar.activation(
+                out=rstd[:, lo:hi], in_=ssum[:, lo:hi], func=ACT.Abs_reciprocal_sqrt, scale=1.0 / N, bias=eps_col[:]
+            )
             if lo == 0:
                 finish(0)
 

from contextlib import ExitStack

import concourse.mybir as mybir
from concourse.masks import make_identity

ROWS, K, N = 512, 1536, 1536
FLOPS = 2 * ROWS * K * N
EPS = 1e-6

F32 = mybir.dt.float32
BF16 = mybir.dt.bfloat16
U32 = mybir.dt.uint32
U8 = mybir.dt.uint8
FP8 = mybir.dt.float8_e4m3fn
FP8X4 = mybir.dt.float8_e4m3fn_x4
ALU = mybir.AluOpType
ACT = mybir.ActivationFunctionType

P = 128
PACK = 4
K_PASS = P * PACK
PASSES = K // K_PASS
HD = 128
HEADS = N // HD
RT = ROWS // P
WIDTHS = (512, 512, 256, 256)
STARTS = tuple(sum(WIDTHS[:c]) for c in range(len(WIDTHS)))
CHUNKS = len(WIDTHS)
UNITS = CHUNKS * PASSES

LOADS = ((0, 512), (512, 1024), (1024, 1536))

X_AT = 2
BG_AT = 2
TAB_AT = 6
SQ_AT = (5, 5, 6, 7, 8, 9, 10, 11, 12, 12, 13, 13)
PROD_AT = (7, 9, 12)
SLOTS = 14

V_WIDEN_EVERY = 6

GROUP = 4
BANKS = RT * HEADS // GROUP
PAIR = 2
LATE = 4
MID = 2
TR_BANKS = 3
MX_BANKS = 4
AHEAD = TR_BANKS + MX_BANKS
READY = RT


def tile_causalwanselfattention_pa_kernel(tc, x, w_bytes, w_scale, b, g, freqs, out):
    nc = tc.nc
    with ExitStack() as ctx:
        const = ctx.enter_context(tc.tile_pool(name="const", bufs=1))
        wide_pool = ctx.enter_context(tc.tile_pool(name="wide", bufs=4))
        grp_pool = ctx.enter_context(tc.tile_pool(name="grp", bufs=3))
        sq_pool = ctx.enter_context(tc.tile_pool(name="sq", bufs=6))
        z_pool = ctx.enter_context(tc.tile_pool(name="z", bufs=3))
        psum_y = ctx.enter_context(tc.psum_pool(name="psy", bufs=MX_BANKS))
        psum_tr = ctx.enter_context(tc.psum_pool(name="pstr", bufs=TR_BANKS))
        psum_s = ctx.enter_context(tc.psum_pool(name="pss", bufs=1))
        ctx.enter_context(tc.manual_schedule())

        wsc = const.tile([P, PASSES, PACK], F32, name="wsc")
        wv = w_bytes.rearrange("(g p t) n -> g p t n", p=P, t=PACK)
        xv = x.rearrange("(t p) k -> p t k", p=P)
        wbytes = [
            [const.tile([P, PACK, hi - lo], U8, name="wbytes%d_%d" % (j, i)) for i in range(PASSES)]
            for j, (lo, hi) in enumerate(LOADS)
        ]
        x_sb = [const.tile([P, 2, K], BF16, name="x_sb%d" % half) for half in range(2)]
        f_sb = const.tile([P, RT, HD], BF16, name="f_sb")
        bg_rows = const.tile([P, P], BF16, name="bg_rows")
        nc.vector.memset(bg_rows[:], 0.0)

        def load_bg():
            for vec, row0 in ((b, 0), (g, 32)):
                vrows = vec.rearrange("(h d) -> h d", d=HD)
                for lo, hi in ((0, 8), (8, HEADS)):
                    nc.sync.dma_start(out=bg_rows[row0 + lo : row0 + hi, :], in_=vrows[lo:hi, :])

        def load_w(j, first=0, end=PASSES):
            lo, hi = LOADS[j]
            for i in range(first, end):
                for t0, t1 in ((0, 2), (2, PACK)) if (j, i) == (0, 0) else ((0, PACK),):
                    nc.sync.dma_start(out=wbytes[j][i][:, t0:t1, :], in_=wv[i][:, t0:t1, lo:hi])

        def load_x(half):
            nc.sync.dma_start(out=x_sb[half][:], in_=xv[:, 2 * half : 2 * half + 2, :])

        nc.sync.dma_start(out=wsc[:], in_=w_scale.rearrange("(g p t) o -> p g (t o)", p=P, t=PACK))
        load_w(0)
        load_bg()
        load_x(0)
        load_w(1, 0, 1)
        load_x(1)
        nc.sync.dma_start(out=f_sb[:], in_=freqs.rearrange("(t p) d -> p t d", p=P))
        load_w(1, 1, PASSES)
        load_w(2)

        warm = const.tile([P, 2], F32, name="warm")
        nc.vector.memset(warm[:], 1.0)
        warm_out = const.tile([P, 2], F32, name="warm_out")
        nc.scalar.activation(out=warm_out[:], in_=warm[:], func=ACT.Abs_reciprocal_sqrt)

        ident_f = const.tile([P, P], F32, name="ident_f")
        make_identity(nc, ident_f[:])
        ident_b = const.tile([P, P], BF16, name="ident_b")
        make_identity(nc, ident_b[:])
        swap_f = const.tile([P, P], F32, name="swap_f")
        iv = ident_f[:].rearrange("p (j e) -> p j e", e=2)
        sw = swap_f[:].rearrange("p (j e) -> p j e", e=2)
        nc.gpsimd.tensor_scalar(out=sw[:, :, 0:1], in0=iv[:, :, 1:2], scalar1=1.0, scalar2=0.0, op0=ALU.mult, op1=ALU.add)
        nc.gpsimd.tensor_scalar(out=sw[:, :, 1:2], in0=iv[:, :, 0:1], scalar1=1.0, scalar2=0.0, op0=ALU.mult, op1=ALU.add)
        sel = [const.tile([P, P], BF16, name="sel%d" % e) for e in range(2)]
        ib = ident_b[:].rearrange("p (j e) -> p j e", e=2)
        for e in range(2):
            se = sel[e][:].rearrange("p (j e) -> p j e", e=2)
            for col in range(2):
                sign = -1.0 if e == 1 and col == 1 else 1.0
                nc.gpsimd.tensor_scalar(
                    out=se[:, :, col : col + 1], in0=ib[:, :, e : e + 1], scalar1=sign, scalar2=0.0, op0=ALU.mult, op1=ALU.add
                )

        xcodes = const.tile([P, PASSES, ROWS], U32, name="xcodes", align_bytes=64)
        xscales = const.tile([P, PASSES, ROWS], U8, name="xscales", align_bytes=64)
        wcodes = const.tile([P, PASSES, N], U32, name="wcodes", align_bytes=64)
        wscales = const.tile([P, PASSES, N], U8, name="wscales", align_bytes=64)

        xgrps = [const.tile([P, ROWS * PACK], BF16, name="xgrp%d" % i, align_bytes=64) for i in range(PASSES)]

        def x_turn(half):
            for i in range(PASSES):
                xt = psum_tr.tile([P, 2, 2 * P], F32, name="xt", tag="tr")
                for u in range(2):
                    for s in range(2):
                        words = x_sb[half][:, s, i * K_PASS : (i + 1) * K_PASS].bitcast(F32)
                        nc.tensor.transpose(xt[:, u, s * P : (s + 1) * P], words[:, u : 2 * P : 2], ident_f[:])
                xgw = xgrps[i][:].bitcast(F32).rearrange("p (r u) -> p r u", u=2)
                dst = xgw[:, 2 * P * half : 2 * P * (half + 1), :]
                src = xt[:].rearrange("p u r -> p r u")
                if half == 0:
                    nc.vector.tensor_copy(out=dst, in_=src)
                else:
                    nc.scalar.copy(out=dst, in_=src)

        def x_quant(i):
            nc.vector.quantize_mx(out=xcodes[:, i, :].bitcast(FP8X4), scales=xscales[:, i, :], in_=xgrps[i][:])

        wides = {}
        wgrps = {}

        def unit_columns(u):
            c, i = divmod(u, PASSES)
            return i, slice(STARTS[c], STARTS[c] + WIDTHS[c])

        def w_widen(u):
            i, cols = unit_columns(u)
            width = cols.stop - cols.start
            j = [n for n, (lo, hi) in enumerate(LOADS) if lo <= cols.start < hi][0]
            c0 = cols.start - LOADS[j][0]
            wide = wide_pool.tile([P, PACK, width], BF16, name="wide", tag="wide")
            wides[u] = wide
            for t in range(PACK):
                codes = wbytes[j][i][:, t, c0 : c0 + width].bitcast(FP8)
                if (u == 0 and t > 0) or (u > 0 and (u * PACK + t + 1) % V_WIDEN_EVERY == 0):
                    nc.vector.tensor_scalar(
                        out=wide[:, t, :], in0=codes, scalar1=wsc[:, i, t : t + 1], scalar2=None, op0=ALU.mult
                    )
                else:
                    nc.scalar.activation(out=wide[:, t, :], in_=codes, func=ACT.Copy, scale=wsc[:, i, t : t + 1])

        def w_weave(u):
            i, cols = unit_columns(u)
            wgrp = grp_pool.tile([P, (cols.stop - cols.start) * PACK], BF16, name="wgrp", tag="wgrp", align_bytes=64)
            wgrps[u] = wgrp
            nc.vector.tensor_copy(
                out=wgrp[:].rearrange("p (c i t) -> p c t i", i=4, t=PACK),
                in_=wides[u][:].rearrange("p t (c i) -> p c t i", i=4),
            )

        def w_quant(u):
            i, cols = unit_columns(u)
            nc.vector.quantize_mx(out=wcodes[:, i, cols].bitcast(FP8X4), scales=wscales[:, i, cols], in_=wgrps[u][:])

        bgc = const.tile([P, 64], F32, name="bgc")
        bg_prod = const.tile([P, HEADS], F32, name="bg_prod")
        tab = const.tile([P, 2, ROWS], BF16, name="tab")
        zcs = {}

        def bias_gain_columns():
            bgt = psum_tr.tile([P, P], BF16, name="bgt", tag="tr")
            nc.tensor.transpose(bgt[:], bg_rows[:], ident_b[:])
            nc.vector.tensor_copy(out=bgc[:], in_=bgt[:, 0:64])
            nc.vector.tensor_tensor(out=bg_prod[:], in0=bgc[:, 0:HEADS], in1=bgc[:, 32 : 32 + HEADS], op=ALU.mult)

        f_turned = const.tile([P, ROWS], BF16, name="f_turned")

        fts = []

        def turn_freqs():
            ft = psum_tr.tile([P, ROWS], BF16, name="ft", tag="tr")
            fts.append(ft)
            for r in range(RT):
                nc.tensor.transpose(ft[:, r * P : (r + 1) * P], f_sb[:, r, :], ident_b[:])

        def copy_freqs():
            nc.vector.tensor_copy(out=f_turned[:], in_=fts[0][:])

        def tables():
            for e in range(2):
                tt = psum_tr.tile([P, ROWS], BF16, name="tt", tag="tr")
                nc.tensor.matmul(out=tt[:], lhsT=sel[e][:], rhs=f_turned[:], start=True, stop=True)
                nc.vector.tensor_copy(out=tab[:, e, :], in_=tt[:])

        ssq = psum_s.tile([P, RT, P], F32, name="ssq")
        out_sb = const.tile([P, RT, N], F32, name="out_sb")
        rstd = const.tile([P, RT], F32, name="rstd")
        ov = out.rearrange("(t p) h d -> t p (h d)", p=P)
        z_late = const.tile([P, LATE, ROWS], F32, name="z_late")
        q_late = [const.tile([P, RT, LATE, P], F32, name="q_late%d" % e) for e in range(2)]
        ys = {}
        ysqs = {}
        q_pair = {}
        qs = {}

        def mx_pass(h, i):
            if i == 0:
                ys[h] = psum_y.tile([P, ROWS], F32, name="y", tag="y")
            hc = slice(h * HD, (h + 1) * HD)
            nc.tensor.matmul_mx(
                out=ys[h][:],
                lhsT=wcodes[:, i, hc].bitcast(FP8X4),
                lhsT_scale=wscales[:, i, hc],
                rhs=xcodes[:, i, :].bitcast(FP8X4),
                rhs_scale=xscales[:, i, :],
                start=(i == 0),
                stop=(i == PASSES - 1),
            )

        def square(h):
            ysq = sq_pool.tile([P, ROWS], F32, name="ysq", tag="ysq")
            ysqs[h] = ysq
            nc.scalar.activation(out=ysq[:], in_=ys[h][:], func=ACT.Square, bias=bgc[:, h : h + 1])

        def gain(h):
            if h < HEADS - LATE:
                if h % PAIR == 0:
                    zcs[h // PAIR] = z_pool.tile([P, PAIR, ROWS], F32, name="z", tag="z")
                z = zcs[h // PAIR][:, h % PAIR, :]
            else:
                z = z_late[:, h - (HEADS - LATE), :]
            gcol, bgcol = bgc[:, 32 + h : 33 + h], bg_prod[:, h : h + 1]
            nc.scalar.activation(out=z, in_=ys[h][:], func=ACT.Identity, scale=gcol, bias=bgcol)

        def products(c, lo=0, hi=ROWS):
            if lo == 0:
                q = const.tile([P, 2, PAIR, ROWS], F32, name="q_%d" % c)
                q_pair[c] = q
                for k in range(PAIR):
                    qs[c * PAIR + k] = [[q[:, e, k, r * P : (r + 1) * P] for r in range(RT)] for e in range(2)]
            nc.vector.tensor_tensor(
                out=q_pair[c][:, :, :, lo:hi],
                in0=zcs[c][:, :, lo:hi].unsqueeze(1).to_broadcast([P, 2, PAIR, hi - lo]),
                in1=tab[:, :, lo:hi].unsqueeze(2).to_broadcast([P, 2, PAIR, hi - lo]),
                op=ALU.mult,
            )

        def late_products(r):
            rows = slice(r * P, (r + 1) * P)
            for e in range(2):
                nc.vector.tensor_tensor(
                    out=q_late[e][:, r, :, :],
                    in0=z_late[:, :, rows],
                    in1=tab[:, e, rows].unsqueeze(1).to_broadcast([P, LATE, P]),
                    op=ALU.mult,
                )

        def sum_squares(h):
            for r in range(RT):
                nc.tensor.matmul(
                    out=ssq[:, r, :],
                    lhsT=ysqs[h][:, r * P : (r + 1) * P],
                    rhs=ident_f[:],
                    is_transpose=True,
                    start=(h == 0 and r == 0),
                    stop=(h == HEADS - 1 and r == RT - 1),
                )

        banks = {}

        def fill(n, first=0, end=GROUP):
            gq, r = divmod(n, RT)
            if first == 0:
                if n == AHEAD:
                    banks[n] = psum_s.tile([P, GROUP, HD], F32, name="bank_s", tag="ssq")
                elif (n - n // (AHEAD + 1)) % AHEAD < TR_BANKS:
                    banks[n] = psum_tr.tile([P, GROUP, HD], F32, name="bank", tag="tr")
                else:
                    banks[n] = psum_y.tile([P, GROUP, HD], F32, name="bank_y", tag="y")
            for k in range(first, end):
                for e, perm in ((0, ident_f), (1, swap_f)):
                    nc.tensor.matmul(
                        out=banks[n][:, k, :],
                        lhsT=qs[gq * GROUP + k][e][r],
                        rhs=perm[:],
                        is_transpose=True,
                        start=(e == 0),
                        stop=(e == 1),
                    )

        def finish(n):
            gq, r = divmod(n, RT)
            for lo, hi in ((0, PAIR), (PAIR, GROUP)) if n == 0 else ((0, GROUP),):
                cols = slice((gq * GROUP + lo) * HD, (gq * GROUP + hi) * HD)
                dst = out_sb[:, r, cols]
                src = banks[n][:, lo:hi, :].rearrange("p k d -> p (k d)")
                if n != BANKS - 1:
                    nc.scalar.activation(out=dst, in_=src, func=ACT.Copy, scale=rstd[:, r : r + 1])
                else:
                    nc.vector.tensor_scalar(out=dst, in0=src, scalar1=rstd[:, r : r + 1], scalar2=None, op0=ALU.mult)
                nc.sync.dma_start(out=ov[r][:, cols], in_=dst)

        ssum = const.tile([P, RT], F32, name="ssum")
        eps_col = const.tile([P, 1], F32, name="eps_col")
        nc.vector.memset(eps_col[:], EPS)

        def chunk_heads(c):
            return range(STARTS[c] // HD, (STARTS[c] + WIDTHS[c]) // HD)

        for u in range(SLOTS):
            if u < UNITS:
                w_widen(u)
            if 0 <= u - 1 < UNITS:
                w_weave(u - 1)
            if u == BG_AT:
                bias_gain_columns()
            if 0 <= u - X_AT < 2:
                x_turn(u - X_AT)
            if 0 <= u - 2 < UNITS - 1 and u - 2 != PASSES - 1:
                w_quant(u - 2)
            if u == X_AT + 1:
                for i in range(PASSES):
                    x_quant(i)
                w_quant(PASSES - 1)
            if u == UNITS:
                w_quant(UNITS - 1)
            if u == TAB_AT - 2:
                turn_freqs()
            if u == TAB_AT - 1:
                copy_freqs()
            if u == TAB_AT:
                tables()
            for c in range(CHUNKS):
                if u == (PASSES * c + PASSES + 1 if c < CHUNKS - 1 else UNITS):
                    if c == 1:
                        for h in chunk_heads(c):
                            for i in range(PASSES):
                                mx_pass(h, i)
                    else:
                        for i in range(PASSES):
                            for h in chunk_heads(c):
                                mx_pass(h, i)
            heads = [h for h in range(HEADS) if SQ_AT[h] == u]
            for h in heads:
                square(h)
            for h in heads:
                gain(h)
            for h in range(HEADS):
                if min(SQ_AT[h] + 1, SLOTS - 1) == u:
                    sum_squares(h)
            for p, at in enumerate(PROD_AT):
                if at == u:
                    products(p)
                    if p == len(PROD_AT) - 1:
                        products(p + 1, 0, P)
            if u == SLOTS - 1:
                products(len(PROD_AT), P, 2 * P)
            if u == PROD_AT[1]:
                for n in range(TR_BANKS):
                    fill(n, 0, PAIR)
            if u == UNITS:
                fill(0, PAIR, GROUP)
        for n in range(1, TR_BANKS):
            fill(n, PAIR, GROUP)
        for n in range(TR_BANKS, READY):
            fill(n)
        filled = READY

        for lo, hi in ((0, 1), (1, RT)):
            nc.vector.tensor_reduce(out=ssum[:, lo:hi], in_=ssq[:, lo:hi, :], axis=mybir.AxisListType.X, op=ALU.add)
            nc.scalar.activation(
                out=rstd[:, lo:hi], in_=ssum[:, lo:hi], func=ACT.Abs_reciprocal_sqrt, scale=1.0 / N, bias=eps_col[:]
            )
            if lo == 0:
                finish(0)

        for h in range(HEADS - LATE, HEADS):
            qs[h] = [[q_late[e][:, r, h - (HEADS - LATE), :] for r in range(RT)] for e in range(2)]
        for r in range(2, RT):
            products(len(PROD_AT), r * P, (r + 1) * P)
        for r in range(RT):
            late_products(r)
        while filled < AHEAD + 1:
            fill(filled)
            filled += 1
        fill(filled)
        filled += 1
        for n in range(1, BANKS):
            finish(n)
            if filled < BANKS:
                fill(filled)
                filled += 1
